import numpy as np
import ml_dtypes


def mxq(x, axis, fmt="e4m3"):
    dtype, down = {"e4m3": (ml_dtypes.float8_e4m3fn, 7), "e5m2": (ml_dtypes.float8_e5m2, 14)}[fmt]
    v = np.moveaxis(np.asarray(x, np.float32).astype(ml_dtypes.bfloat16).astype(np.float64), axis, -1)
    blocks = v.reshape(v.shape[:-1] + (-1, 32))
    amax = np.abs(blocks).max(-1, keepdims=True)
    byte = np.maximum(np.where(amax > 0, np.frexp(amax)[1] - 1 + 127, 0) - down, 1)
    scale = np.exp2(byte - 127.0)
    codes = (blocks / scale).astype(np.float32).astype(dtype).astype(np.float64)
    return np.moveaxis((codes * scale).reshape(v.shape), -1, axis)


WIDE = False


def mx_kscale(k):
    if not WIDE:
        return np.ones(k)
    levels = np.array([10, -10, 5, -5, 0])
    if k % 512:
        return np.exp2(np.random.permutation(np.resize(levels, k // 32))).repeat(32)
    a = np.empty((k // 512, 16))
    for p in range(k // 512):
        a[p, :8] = np.random.permutation(np.resize(levels, 8))
        for g in range(8):
            far = levels[np.abs(levels - a[p, g]) >= 10]
            a[p, g + 8] = far[np.random.randint(len(far))]
    return np.exp2(a.ravel()).repeat(32)


BF16 = ml_dtypes.bfloat16


def bf(x):
    return np.asarray(x, np.float32).astype(BF16)


def f64(x):
    return np.asarray(x).astype(np.float64)


B, T, HID, H, D, QB = 4, 1024, 1024, 4, 128, 512
LN_EPS = 1e-5


def layer_norm(u):
    mu = u.mean(-1, keepdims=True)
    var = ((u - mu) ** 2).mean(-1, keepdims=True)
    return (u - mu) * (1.0 / np.sqrt(var + LN_EPS))


def feature_map(u, gamma, beta):
    return layer_norm(u * gamma + beta)


def setup_inputs():
    s = mx_kscale(HID)
    return {"hidden_states": bf(np.random.standard_normal((B, T, HID)) * s),
            "Wq": bf(np.random.standard_normal((H * D, HID)) / np.sqrt(HID) / s),
            "Wk": bf(np.random.standard_normal((H * D, HID)) / np.sqrt(HID) / s),
            "gamma": bf(1.0 + 0.1 * np.random.standard_normal(D)),
            "beta": bf(0.1 * np.random.standard_normal(D))}


def reference(hidden_states, Wq, Wk, gamma, beta):
    g, b = f64(gamma), f64(beta)
    xq = mxq(f64(hidden_states), 2, "e4m3")
    q = (xq @ mxq(f64(Wq), 1, "e4m3").T).reshape(B, T, H, D)
    k = (xq @ mxq(f64(Wk), 1, "e4m3").T).reshape(B, T, H, D)
    q_feat = feature_map(q, g, b) * (D ** -0.5)
    k_feat = feature_map(k, g, b)
    return q_feat, k_feat

@@ -1,0 +1,271 @@
+from contextlib import ExitStack
+
+import concourse.mybir as mybir
+from concourse.masks import make_identity
+
+F32 = mybir.dt.float32
+BF16 = mybir.dt.bfloat16
+U32 = mybir.dt.uint32
+U8 = mybir.dt.uint8
+FP8X4 = mybir.dt.float8_e4m3fn_x4
+ALU = mybir.AluOpType
+ACT = mybir.ActivationFunctionType
+
+P = 128
+TOKENS = 4 * 1024
+HID = 1024
+HEADS = 4
+D = 128
+LN_EPS = 1e-5
+K_PASS = 4 * P
+PASSES = HID // K_PASS
+WORDS = K_PASS // 2
+GROUP = 512
+N_GROUPS = TOKENS // GROUP
+TILES = GROUP // P
+N_BLOCKS = 2 * N_GROUPS
+ROWS = TILES * HEADS
+RUN = 2
+ROUNDS = HEADS // RUN
+N_ROUNDS = N_BLOCKS * ROUNDS
+JOBS_FIRST = 8
+JOBS_PER_ROUND = 3
+
+FLOPS = 2 * TOKENS * HID * 2 * HEADS * D
+
+
+def tile_rebasedlinearattention_pa_t_kernel(tc, hidden_states, Wq, Wk, gamma, beta, out_0, out_1):
+    nc = tc.nc
+    x_dram = hidden_states.rearrange("b t k -> (b t) k").rearrange("(g p t) k -> g p t k", p=P, t=TILES)
+    w_dram = [w.rearrange("(h p) k -> p h k", p=P) for w in (Wq, Wk)]
+    out_dram = [
+        o.rearrange("b t h d -> (b t) (h d)").rearrange("(g p t) f -> g p t f", p=P, t=TILES) for o in (out_0, out_1)
+    ]
+
+    with ExitStack() as stack:
+        const = stack.enter_context(tc.tile_pool(name="const", bufs=1))
+        raw_pool = stack.enter_context(tc.tile_pool(name="raw", bufs=10))
+        grouped_pool = stack.enter_context(tc.tile_pool(name="grouped", bufs=6))
+        ut_pool = stack.enter_context(tc.tile_pool(name="ut", bufs=2))
+        u_pool = stack.enter_context(tc.tile_pool(name="u", bufs=4))
+        f_pool = stack.enter_context(tc.tile_pool(name="f", bufs=8))
+        small = stack.enter_context(tc.tile_pool(name="small", bufs=3))
+        kt_psum = stack.enter_context(tc.psum_pool(name="kt", bufs=3))
+        mx_psum = stack.enter_context(tc.psum_pool(name="mx", bufs=2))
+        bt_psum = stack.enter_context(tc.psum_pool(name="bt", bufs=3))
+        stack.enter_context(tc.manual_schedule())
+
+        w_codes = const.tile([P, PASSES, 2 * HEADS * D], U32, align_bytes=64)
+        w_scales = const.tile([P, PASSES, 2 * HEADS * D], U8, align_bytes=64)
+        x_codes = const.tile([P, N_GROUPS, PASSES, GROUP], U32, align_bytes=64)
+        x_scales = const.tile([P, N_GROUPS, PASSES, GROUP], U8, align_bytes=64)
+
+        jobs = []
+
+        def load_rows(rows_dram, codes, scales):
+            raw = raw_pool.tile([P, 2, HID], BF16, name="raw")
+            nc.sync.dma_start(out=raw[:], in_=rows_dram)
+            for c in range(PASSES):
+                jobs.append((raw[:].bitcast(F32), c, codes[:, c, :], scales[:, c, :]))
+
+        def load_tokens(g):
+            for t in range(0, TILES, 2):
+                cols = slice(t * P, (t + 2) * P)
+                load_rows(x_dram[g][:, t : t + 2, :], x_codes[:, g, :, cols], x_scales[:, g, :, cols])
+
+        def load_weights(s):
+            for h in range(0, HEADS, 2):
+                cols = slice((s * HEADS + h) * D, (s * HEADS + h + 2) * D)
+                load_rows(w_dram[s][:, h : h + 2, :], w_codes[:, :, cols], w_scales[:, :, cols])
+
+        load_tokens(0)
+        load_weights(0)
+        gb_rows = const.tile([P, P], BF16)
+        nc.vector.memset(gb_rows[:], 0.0)
+        nc.sync.dma_start(out=gb_rows[0:1, :], in_=gamma.rearrange("(o d) -> o d", o=1))
+        nc.sync.dma_start(out=gb_rows[1:2, :], in_=beta.rearrange("(o d) -> o d", o=1))
+        load_weights(1)
+        for g in range(1, N_GROUPS):
+            load_tokens(g)
+
+        ident = const.tile([P, P], F32)
+        make_identity(nc, ident[:])
+        eps_col = const.tile([P, 2], F32)
+        nc.vector.memset(eps_col[:, 0:1], D * LN_EPS)
+        nc.vector.memset(eps_col[:, 1:2], LN_EPS)
+        warm = const.tile([P, 1], F32)
+        nc.scalar.activation(out=warm[:], in_=eps_col[:, 0:1], func=ACT.Abs_reciprocal_sqrt)
+
+        job_bank = {}
+        job_grouped = {}
+
+        def job_transpose(n):
+            words, c, codes, scales = jobs[n]
+            job_bank[n] = kt_psum.tile([P, 2, 2 * P], F32, name="kt")
+            for u in range(2):
+                for r in range(2):
+                    every_second = slice(c * WORDS + u, (c + 1) * WORDS, 2)
+                    nc.tensor.transpose(job_bank[n][:, u, r * P : (r + 1) * P], words[:, r, every_second], ident[:])
+
+        def job_group(n):
+            job_grouped[n] = grouped_pool.tile([P, 2 * P, 4], BF16, align_bytes=64, name="grouped")
+            engine_copy = nc.vector.tensor_copy if n % 2 == 0 else nc.scalar.copy
+            engine_copy(out=job_grouped[n][:].bitcast(F32), in_=job_bank[n][:].rearrange("p u r -> p r u"))
+
+        def job_quantise(n):
+            words, c, codes, scales = jobs[n]
+            nc.vector.quantize_mx(
+                out=codes.bitcast(FP8X4), scales=scales, in_=job_grouped[n][:].rearrange("p r t -> p (r t)")
+            )
+
+        u_t = {}
+        u_sb = {}
+        u_rows = {}
+        stats = {}
+        mean = {}
+        m2 = {}
+        rstd = {}
+
+        def project(block, first_head):
+            g, s = divmod(block, 2)
+            if first_head == 0:
+                u_t[block] = ut_pool.tile([P, HEADS, GROUP], F32, name="u_t")
+            for h in range(first_head, first_head + RUN):
+                cols = slice((s * HEADS + h) * D, (s * HEADS + h + 1) * D)
+                acc = mx_psum.tile([P, GROUP], F32, name="acc")
+                for c in range(PASSES):
+                    nc.tensor.matmul_mx(
+                        out=acc[:],
+                        lhsT=w_codes[:, c, cols].bitcast(FP8X4),
+                        lhsT_scale=w_scales[:, c, cols],
+                        rhs=x_codes[:, g, c, :].bitcast(FP8X4),
+                        rhs_scale=x_scales[:, g, c, :],
+                        start=(c == 0),
+                        stop=(c == PASSES - 1),
+                    )
+                nc.scalar.activation(
+                    out=u_t[block][:, h, :], in_=acc[:], func=ACT.Identity, scale=gb_col[:, 0:1], bias=gb_col[:, 1:2]
+                )
+
+        def tokens_to_partitions(block, first_tile, jobs_are_done):
+            if first_tile == 0:
+                u_sb[block] = u_pool.tile([P, TILES, HEADS * D], F32, name="u_sb")
+            for t in range(first_tile, first_tile + RUN):
+                stays = jobs_are_done and t == TILES - 1
+                if stays:
+                    bank = kt_psum.tile([P, HEADS * D], F32, name="kt")
+                else:
+                    bank = bt_psum.tile([P, HEADS * D], F32, name="bank")
+                for h in range(HEADS):
+                    nc.tensor.transpose(bank[:, h * D : (h + 1) * D], u_t[block][:, h, t * P : (t + 1) * P], ident[:])
+                if stays:
+                    u_rows[block, t] = bank
+                else:
+                    nc.scalar.copy(out=u_sb[block][:, t, :], in_=bank[:])
+                    u_rows[block, t] = u_sb[block][:, t, :]
+
+        def statistics(block, first_tile):
+            if first_tile == 0:
+                stats[block] = small.tile([P, ROWS, 6], F32, name="stats")
+            for t in range(first_tile, first_tile + RUN):
+                for h in range(HEADS):
+                    nc.vector.bn_stats(out=stats[block][:, t * HEADS + h, :], in_=u_rows[block, t][:, h * D : (h + 1) * D])
+
+        def merge_halves(block):
+            halves = stats[block][:].rearrange("p n (e k) -> p n e k", e=2)
+            gap = small.tile([P, ROWS], F32, name="gap")
+            nc.gpsimd.tensor_sub(out=gap[:], in0=halves[:, :, 0, 1], in1=halves[:, :, 1, 1])
+            within = small.tile([P, ROWS], F32, name="within")
+            nc.gpsimd.tensor_add(out=within[:], in0=halves[:, :, 0, 2], in1=halves[:, :, 1, 2])
+            gap_scaled = small.tile([P, ROWS], F32, name="gap_scaled")
+            nc.gpsimd.tensor_scalar(
+                out=gap_scaled[:], in0=gap[:], scalar1=D / 4.0, scalar2=0.0, op0=ALU.mult, op1=ALU.add
+            )
+            between = small.tile([P, ROWS], F32, name="between")
+            nc.gpsimd.tensor_mul(out=between[:], in0=gap_scaled[:], in1=gap[:])
+            m2[block] = small.tile([P, ROWS], F32, name="m2")
+            nc.gpsimd.tensor_add(out=m2[block][:], in0=between[:], in1=within[:])
+            mean_sum = small.tile([P, ROWS], F32, name="mean_sum")
+            nc.gpsimd.tensor_add(out=mean_sum[:], in0=halves[:, :, 0, 1], in1=halves[:, :, 1, 1])
+            mean[block] = small.tile([P, ROWS], F32, name="mean")
+            nc.gpsimd.tensor_scalar(
+                out=mean[block][:], in0=mean_sum[:], scalar1=0.5, scalar2=0.0, op0=ALU.mult, op1=ALU.add
+            )
+
+        def inverse_deviation(block):
+            s = block % 2
+            rstd[block] = small.tile([P, ROWS], F32, name="rstd")
+            nc.scalar.activation(
+                out=rstd[block][:],
+                in_=m2[block][:],
+                func=ACT.Abs_reciprocal_sqrt,
+                scale=(1.0 if s == 0 else 1.0 / D),
+                bias=eps_col[:, s : s + 1],
+            )
+
+        def normalise(block, first_tile):
+            g, s = divmod(block, 2)
+            for t in range(first_tile, first_tile + RUN):
+                f_sb = f_pool.tile([P, HEADS * D], F32, name="f_sb")
+                for h in range(HEADS):
+                    n = t * HEADS + h
+                    nc.vector.tensor_scalar(
+                        out=f_sb[:, h * D : (h + 1) * D],
+                        in0=u_rows[block, t][:, h * D : (h + 1) * D],
+                        scalar1=mean[block][:, n : n + 1],
+                        scalar2=rstd[block][:, n : n + 1],
+                        op0=ALU.subtract,
+                        op1=ALU.mult,
+                    )
+                nc.sync.dma_start(out=out_dram[s][g][:, t, :], in_=f_sb[:])
+
+        for n in range(JOBS_FIRST):
+            job_transpose(n)
+            job_group(n)
+            if n > 0:
+                job_quantise(n - 1)
+        gb_f32 = const.tile([P, P], F32)
+        nc.vector.tensor_copy(out=gb_f32[:], in_=gb_rows[:])
+        gb_bank = kt_psum.tile([P, 2, 2 * P], F32, name="kt")
+        nc.tensor.transpose(gb_bank[:, 0, 0:P], gb_f32[:], ident[:])
+        gb_col = const.tile([P, 2], F32)
+        nc.vector.tensor_copy(out=gb_col[:], in_=gb_bank[:, 0, 0:2])
+
+        def part_of_block(r):
+            if 0 <= r < N_ROUNDS:
+                return r // ROUNDS, (r % ROUNDS) * RUN
+            return None
+
+        def whole_block(r):
+            if 0 <= r < N_ROUNDS and r % ROUNDS == 0:
+                return r // ROUNDS
+            return None
+
+        done = JOBS_FIRST
+        quantised = JOBS_FIRST - 1
+        for j in range(N_ROUNDS + 7):
+            fresh = range(done, min(done + JOBS_PER_ROUND, len(jobs)))
+            if whole_block(j - 6) is not None:
+                inverse_deviation(whole_block(j - 6))
+            if part_of_block(j) is not None:
+                project(*part_of_block(j))
+            if part_of_block(j - 2) is not None:
+                tokens_to_partitions(*part_of_block(j - 2), len(fresh) == 0)
+            for n in fresh:
+                job_transpose(n)
+            for n in fresh:
+                if n % 2 == 1:
+                    job_group(n)
+            for n in range(quantised, done):
+                job_quantise(n)
+            quantised = done
+            done = done + len(fresh)
+            if part_of_block(j - 3) is not None:
+                statistics(*part_of_block(j - 3))
+            if whole_block(j - 4) is not None:
+                merge_halves(whole_block(j - 4))
+            for n in fresh:
+                if n % 2 == 0:
+                    job_group(n)
+            if part_of_block(j - 7) is not None:
+                normalise(*part_of_block(j - 7))

@@ -122,8 +122,6 @@ def tile_rebasedlinearattention_pa_t_kernel(tc, hidden_states, Wq, Wk, gamma, be
         u_sb = {}
         u_rows = {}
         stats = {}
-        mean = {}
-        m2 = {}
         rstd = {}
 
         def project(block, first_head):
@@ -166,38 +164,23 @@ def tile_rebasedlinearattention_pa_t_kernel(tc, hidden_states, Wq, Wk, gamma, be
 
         def statistics(block, first_tile):
             if first_tile == 0:
-                stats[block] = small.tile([P, ROWS, 6], F32, name="stats")
+                stats[block] = small.tile([P, ROWS, 3], F32, name="stats")
             for t in range(first_tile, first_tile + RUN):
-                for h in range(HEADS):
-                    nc.vector.bn_stats(out=stats[block][:, t * HEADS + h, :], in_=u_rows[block, t][:, h * D : (h + 1) * D])
+                for h in range(0, HEADS, 2):
+                    n = t * HEADS + h
+                    nc.vector.bn_stats(
+                        out=stats[block][:, n : n + 2, :].rearrange("p n k -> p (n k)"),
+                        in_=u_rows[block, t][:, h * D : (h + 2) * D].rearrange("p (h d) -> p d h", h=2),
+                    )
 
-        def merge_halves(block):
-            halves = stats[block][:].rearrange("p n (e k) -> p n e k", e=2)
-            gap = small.tile([P, ROWS], F32, name="gap")
-            nc.gpsimd.tensor_sub(out=gap[:], in0=halves[:, :, 0, 1], in1=halves[:, :, 1, 1])
-            within = small.tile([P, ROWS], F32, name="within")
-            nc.gpsimd.tensor_add(out=within[:], in0=halves[:, :, 0, 2], in1=halves[:, :, 1, 2])
-            gap_scaled = small.tile([P, ROWS], F32, name="gap_scaled")
-            nc.gpsimd.tensor_scalar(
-                out=gap_scaled[:], in0=gap[:], scalar1=D / 4.0, scalar2=0.0, op0=ALU.mult, op1=ALU.add
-            )
-            between = small.tile([P, ROWS], F32, name="between")
-            nc.gpsimd.tensor_mul(out=between[:], in0=gap_scaled[:], in1=gap[:])
-            m2[block] = small.tile([P, ROWS], F32, name="m2")
-            nc.gpsimd.tensor_add(out=m2[block][:], in0=between[:], in1=within[:])
-            mean_sum = small.tile([P, ROWS], F32, name="mean_sum")
-            nc.gpsimd.tensor_add(out=mean_sum[:], in0=halves[:, :, 0, 1], in1=halves[:, :, 1, 1])
-            mean[block] = small.tile([P, ROWS], F32, name="mean")
-            nc.gpsimd.tensor_scalar(
-                out=mean[block][:], in0=mean_sum[:], scalar1=0.5, scalar2=0.0, op0=ALU.mult, op1=ALU.add
-            )
-
-        def inverse_deviation(block):
+        def inverse_deviation(block, first_tile):
             s = block % 2
-            rstd[block] = small.tile([P, ROWS], F32, name="rstd")
+            if first_tile == 0:
+                rstd[block] = small.tile([P, ROWS], F32, name="rstd")
+            rows = slice(first_tile * HEADS, (first_tile + RUN) * HEADS)
             nc.scalar.activation(
-                out=rstd[block][:],
-                in_=m2[block][:],
+                out=rstd[block][:, rows],
+                in_=stats[block][:, rows, 2],
                 func=ACT.Abs_reciprocal_sqrt,
                 scale=(1.0 if s == 0 else 1.0 / D),
                 bias=eps_col[:, s : s + 1],
@@ -212,7 +195,7 @@ def tile_rebasedlinearattention_pa_t_kernel(tc, hidden_states, Wq, Wk, gamma, be
                     nc.vector.tensor_scalar(
                         out=f_sb[:, h * D : (h + 1) * D],
                         in0=u_rows[block, t][:, h * D : (h + 1) * D],
-                        scalar1=mean[block][:, n : n + 1],
+                        scalar1=stats[block][:, n, 1:2],
                         scalar2=rstd[block][:, n : n + 1],
                         op0=ALU.subtract,
                         op1=ALU.mult,
@@ -236,17 +219,12 @@ def tile_rebasedlinearattention_pa_t_kernel(tc, hidden_states, Wq, Wk, gamma, be
                 return r // ROUNDS, (r % ROUNDS) * RUN
             return None
 
-        def whole_block(r):
-            if 0 <= r < N_ROUNDS and r % ROUNDS == 0:
-                return r // ROUNDS
-            return None
-
         done = JOBS_FIRST
         quantised = JOBS_FIRST - 1
-        for j in range(N_ROUNDS + 7):
+        for j in range(N_ROUNDS + 4):
             fresh = range(done, min(done + JOBS_PER_ROUND, len(jobs)))
-            if whole_block(j - 6) is not None:
-                inverse_deviation(whole_block(j - 6))
+            if part_of_block(j - 4) is not None:
+                inverse_deviation(*part_of_block(j - 4))
             if part_of_block(j) is not None:
                 project(*part_of_block(j))
             if part_of_block(j - 2) is not None:
@@ -262,10 +240,8 @@ def tile_rebasedlinearattention_pa_t_kernel(tc, hidden_states, Wq, Wk, gamma, be
             done = done + len(fresh)
             if part_of_block(j - 3) is not None:
                 statistics(*part_of_block(j - 3))
-            if whole_block(j - 4) is not None:
-                merge_halves(whole_block(j - 4))
             for n in fresh:
                 if n % 2 == 0:
                     job_group(n)
-            if part_of_block(j - 7) is not None:
-                normalise(*part_of_block(j - 7))
+            if part_of_block(j - 4) is not None:
+                normalise(*part_of_block(j - 4))

@@ -16,6 +16,7 @@ TOKENS = 4 * 1024
 HID = 1024
 HEADS = 4
 D = 128
+F = HEADS * D
 LN_EPS = 1e-5
 K_PASS = 4 * P
 PASSES = HID // K_PASS
@@ -23,15 +24,14 @@ WORDS = K_PASS // 2
 GROUP = 512
 N_GROUPS = TOKENS // GROUP
 TILES = GROUP // P
-N_BLOCKS = 2 * N_GROUPS
-ROWS = TILES * HEADS
-RUN = 2
-ROUNDS = HEADS // RUN
-N_ROUNDS = N_BLOCKS * ROUNDS
+N_TILES = N_GROUPS * TILES
+Q_LAG = 3
 JOBS_FIRST = 8
-JOBS_PER_ROUND = 3
+EARLY_ROUNDS = 3
+JOBS_EARLY = 3
+K_VECTOR = 2
 
-FLOPS = 2 * TOKENS * HID * 2 * HEADS * D
+FLOPS = 2 * TOKENS * HID * 2 * F
 
 
 def tile_rebasedlinearattention_pa_t_kernel(tc, hidden_states, Wq, Wk, gamma, beta, out_0, out_1):
@@ -44,19 +44,19 @@ def tile_rebasedlinearattention_pa_t_kernel(tc, hidden_states, Wq, Wk, gamma, be
 
     with ExitStack() as stack:
         const = stack.enter_context(tc.tile_pool(name="const", bufs=1))
-        raw_pool = stack.enter_context(tc.tile_pool(name="raw", bufs=10))
+        raw_pool = stack.enter_context(tc.tile_pool(name="raw", bufs=20))
         grouped_pool = stack.enter_context(tc.tile_pool(name="grouped", bufs=6))
         ut_pool = stack.enter_context(tc.tile_pool(name="ut", bufs=2))
-        u_pool = stack.enter_context(tc.tile_pool(name="u", bufs=4))
-        f_pool = stack.enter_context(tc.tile_pool(name="f", bufs=8))
-        small = stack.enter_context(tc.tile_pool(name="small", bufs=3))
-        kt_psum = stack.enter_context(tc.psum_pool(name="kt", bufs=3))
-        mx_psum = stack.enter_context(tc.psum_pool(name="mx", bufs=2))
+        uk_pool = stack.enter_context(tc.tile_pool(name="uk", bufs=4))
+        f_pool = stack.enter_context(tc.tile_pool(name="f", bufs=6))
+        small = stack.enter_context(tc.tile_pool(name="small", bufs=4))
+        kt_psum = stack.enter_context(tc.psum_pool(name="kt", bufs=2))
+        mx_psum = stack.enter_context(tc.psum_pool(name="mx", bufs=3))
         bt_psum = stack.enter_context(tc.psum_pool(name="bt", bufs=3))
         stack.enter_context(tc.manual_schedule())
 
-        w_codes = const.tile([P, PASSES, 2 * HEADS * D], U32, align_bytes=64)
-        w_scales = const.tile([P, PASSES, 2 * HEADS * D], U8, align_bytes=64)
+        w_codes = const.tile([P, PASSES, 2 * F], U32, align_bytes=64)
+        w_scales = const.tile([P, PASSES, 2 * F], U8, align_bytes=64)
         x_codes = const.tile([P, N_GROUPS, PASSES, GROUP], U32, align_bytes=64)
         x_scales = const.tile([P, N_GROUPS, PASSES, GROUP], U8, align_bytes=64)
 
@@ -68,28 +68,31 @@ def tile_rebasedlinearattention_pa_t_kernel(tc, hidden_states, Wq, Wk, gamma, be
             for c in range(PASSES):
                 jobs.append((raw[:].bitcast(F32), c, codes[:, c, :], scales[:, c, :]))
 
-        def load_tokens(g):
-            for t in range(0, TILES, 2):
-                cols = slice(t * P, (t + 2) * P)
-                load_rows(x_dram[g][:, t : t + 2, :], x_codes[:, g, :, cols], x_scales[:, g, :, cols])
+        def load_tokens(g, t):
+            cols = slice(t * P, (t + 2) * P)
+            load_rows(x_dram[g][:, t : t + 2, :], x_codes[:, g, :, cols], x_scales[:, g, :, cols])
 
         def load_weights(s):
             for h in range(0, HEADS, 2):
                 cols = slice((s * HEADS + h) * D, (s * HEADS + h + 2) * D)
                 load_rows(w_dram[s][:, h : h + 2, :], w_codes[:, :, cols], w_scales[:, :, cols])
 
-        load_tokens(0)
-        load_weights(0)
-        gb_rows = const.tile([P, P], BF16)
-        nc.vector.memset(gb_rows[:], 0.0)
-        nc.sync.dma_start(out=gb_rows[0:1, :], in_=gamma.rearrange("(o d) -> o d", o=1))
-        nc.sync.dma_start(out=gb_rows[1:2, :], in_=beta.rearrange("(o d) -> o d", o=1))
+        gb_row = const.tile([P, 2 * D], BF16)
+        nc.vector.memset(gb_row[:], 0.0)
+        load_tokens(0, 0)
+        nc.sync.dma_start(out=gb_row[0:1, 0:D], in_=gamma.rearrange("(o d) -> o d", o=1))
+        nc.sync.dma_start(out=gb_row[0:1, D : 2 * D], in_=beta.rearrange("(o d) -> o d", o=1))
         load_weights(1)
+        load_tokens(0, 2)
+        load_weights(0)
         for g in range(1, N_GROUPS):
-            load_tokens(g)
+            load_tokens(g, 0)
+            load_tokens(g, 2)
 
         ident = const.tile([P, P], F32)
         make_identity(nc, ident[:])
+        ones = const.tile([P, P], BF16)
+        nc.vector.memset(ones[:], 1.0)
         eps_col = const.tile([P, 2], F32)
         nc.vector.memset(eps_col[:, 0:1], D * LN_EPS)
         nc.vector.memset(eps_col[:, 1:2], LN_EPS)
@@ -99,17 +102,16 @@ def tile_rebasedlinearattention_pa_t_kernel(tc, hidden_states, Wq, Wk, gamma, be
         job_bank = {}
         job_grouped = {}
 
-        def job_transpose(n):
+        def job_transpose(n, pool, name):
             words, c, codes, scales = jobs[n]
-            job_bank[n] = kt_psum.tile([P, 2, 2 * P], F32, name="kt")
+            job_bank[n] = pool.tile([P, 2, 2 * P], F32, name=name)
             for u in range(2):
                 for r in range(2):
                     every_second = slice(c * WORDS + u, (c + 1) * WORDS, 2)
                     nc.tensor.transpose(job_bank[n][:, u, r * P : (r + 1) * P], words[:, r, every_second], ident[:])
 
-        def job_group(n):
+        def job_group(n, engine_copy):
             job_grouped[n] = grouped_pool.tile([P, 2 * P, 4], BF16, align_bytes=64, name="grouped")
-            engine_copy = nc.vector.tensor_copy if n % 2 == 0 else nc.scalar.copy
             engine_copy(out=job_grouped[n][:].bitcast(F32), in_=job_bank[n][:].rearrange("p u r -> p r u"))
 
         def job_quantise(n):
@@ -118,130 +120,179 @@ def tile_rebasedlinearattention_pa_t_kernel(tc, hidden_states, Wq, Wk, gamma, be
                 out=codes.bitcast(FP8X4), scales=scales, in_=job_grouped[n][:].rearrange("p r t -> p (r t)")
             )
 
-        u_t = {}
-        u_sb = {}
-        u_rows = {}
-        stats = {}
-        rstd = {}
+        job_pools = [(kt_psum, "kt"), (kt_psum, "kt"), (bt_psum, "bank")]
+        for n in range(JOBS_FIRST):
+            job_transpose(n, *job_pools[n % 3])
+            job_group(n, nc.vector.tensor_copy if n % 2 == 0 else nc.scalar.copy)
+            if n > 0:
+                job_quantise(n - 1)
+        job_quantise(JOBS_FIRST - 1)
+        gb_bank = bt_psum.tile([P, F], F32, name="bank")
+        nc.tensor.matmul(out=gb_bank[:, 0 : 2 * D], lhsT=ones[:], rhs=gb_row[:], start=True, stop=True)
+        gamma_all = const.tile([P, HEADS, D], F32)
+        beta_all = const.tile([P, HEADS, D], F32)
+        for h in range(HEADS):
+            nc.scalar.copy(out=gamma_all[:, h, :], in_=gb_bank[:, 0:D])
+            nc.scalar.copy(out=beta_all[:, h, :], in_=gb_bank[:, D : 2 * D])
+        col_bank = bt_psum.tile([P, F], F32, name="bank")
+        nc.tensor.transpose(col_bank[:, 0:P], gamma_all[:, 0, :], ident[:])
+        nc.tensor.transpose(col_bank[:, P : 2 * P], beta_all[:, 0, :], ident[:])
+        gb_col = const.tile([P, 2], F32)
+        nc.scalar.copy(out=gb_col[:, 0:1], in_=col_bank[:, 0:1])
+        nc.scalar.copy(out=gb_col[:, 1:2], in_=col_bank[:, P : P + 1])
 
-        def project(block, first_head):
-            g, s = divmod(block, 2)
-            if first_head == 0:
-                u_t[block] = ut_pool.tile([P, HEADS, GROUP], F32, name="u_t")
-            for h in range(first_head, first_head + RUN):
-                cols = slice((s * HEADS + h) * D, (s * HEADS + h + 1) * D)
-                acc = mx_psum.tile([P, GROUP], F32, name="acc")
-                for c in range(PASSES):
-                    nc.tensor.matmul_mx(
-                        out=acc[:],
-                        lhsT=w_codes[:, c, cols].bitcast(FP8X4),
-                        lhsT_scale=w_scales[:, c, cols],
-                        rhs=x_codes[:, g, c, :].bitcast(FP8X4),
-                        rhs_scale=x_scales[:, g, c, :],
-                        start=(c == 0),
-                        stop=(c == PASSES - 1),
-                    )
-                nc.scalar.activation(
-                    out=u_t[block][:, h, :], in_=acc[:], func=ACT.Identity, scale=gb_col[:, 0:1], bias=gb_col[:, 1:2]
+        k_acc = {}
+        u_k = {}
+
+        def project_k(i):
+            g, t = divmod(i, TILES)
+            rows = slice(t * P, (t + 1) * P)
+            k_acc[i] = mx_psum.tile([P, F], F32, name="acc")
+            for c in range(PASSES):
+                nc.tensor.matmul_mx(
+                    out=k_acc[i][:],
+                    lhsT=x_codes[:, g, c, rows].bitcast(FP8X4),
+                    lhsT_scale=x_scales[:, g, c, rows],
+                    rhs=w_codes[:, c, F : 2 * F].bitcast(FP8X4),
+                    rhs_scale=w_scales[:, c, F : 2 * F],
+                    start=(c == 0),
+                    stop=(c == PASSES - 1),
                 )
 
-        def tokens_to_partitions(block, first_tile, jobs_are_done):
-            if first_tile == 0:
-                u_sb[block] = u_pool.tile([P, TILES, HEADS * D], F32, name="u_sb")
-            for t in range(first_tile, first_tile + RUN):
-                stays = jobs_are_done and t == TILES - 1
-                if stays:
-                    bank = kt_psum.tile([P, HEADS * D], F32, name="kt")
-                else:
-                    bank = bt_psum.tile([P, HEADS * D], F32, name="bank")
-                for h in range(HEADS):
-                    nc.tensor.transpose(bank[:, h * D : (h + 1) * D], u_t[block][:, h, t * P : (t + 1) * P], ident[:])
-                if stays:
-                    u_rows[block, t] = bank
-                else:
-                    nc.scalar.copy(out=u_sb[block][:, t, :], in_=bank[:])
-                    u_rows[block, t] = u_sb[block][:, t, :]
+        def affine_k(i):
+            scaled = uk_pool.tile([P, F], F32, name="scaled")
+            nc.vector.tensor_mul(out=scaled[:], in0=k_acc[i][:], in1=gamma_all[:].rearrange("p h d -> p (h d)"))
+            u_k[i] = uk_pool.tile([P, F], F32, name="u_k")
+            nc.gpsimd.tensor_add(out=u_k[i][:], in0=scaled[:], in1=beta_all[:].rearrange("p h d -> p (h d)"))
 
-        def statistics(block, first_tile):
-            if first_tile == 0:
-                stats[block] = small.tile([P, ROWS, 3], F32, name="stats")
-            for t in range(first_tile, first_tile + RUN):
-                for h in range(0, HEADS, 2):
-                    n = t * HEADS + h
-                    nc.vector.bn_stats(
-                        out=stats[block][:, n : n + 2, :].rearrange("p n k -> p (n k)"),
-                        in_=u_rows[block, t][:, h * D : (h + 2) * D].rearrange("p (h d) -> p d h", h=2),
-                    )
+        q_t = {}
+        u_q = {}
 
-        def inverse_deviation(block, first_tile):
-            s = block % 2
-            if first_tile == 0:
-                rstd[block] = small.tile([P, ROWS], F32, name="rstd")
-            rows = slice(first_tile * HEADS, (first_tile + RUN) * HEADS)
+        def project_q(i):
+            g, h = divmod(i, HEADS)
+            if h == 0:
+                q_t[g] = ut_pool.tile([P, HEADS, GROUP], F32, name="q_t")
+            cols = slice(h * D, (h + 1) * D)
+            acc = mx_psum.tile([P, GROUP], F32, name="acc")
+            for c in range(PASSES):
+                nc.tensor.matmul_mx(
+                    out=acc[:],
+                    lhsT=w_codes[:, c, cols].bitcast(FP8X4),
+                    lhsT_scale=w_scales[:, c, cols],
+                    rhs=x_codes[:, g, c, :].bitcast(FP8X4),
+                    rhs_scale=x_scales[:, g, c, :],
+                    start=(c == 0),
+                    stop=(c == PASSES - 1),
+                )
             nc.scalar.activation(
-                out=rstd[block][:, rows],
-                in_=stats[block][:, rows, 2],
+                out=q_t[g][:, h, :], in_=acc[:], func=ACT.Identity, scale=gb_col[:, 0:1], bias=gb_col[:, 1:2]
+            )
+
+        def transpose_back_q(i):
+            g, t = divmod(i, TILES)
+            u_q[i] = bt_psum.tile([P, F], F32, name="bank")
+            for h in range(HEADS):
+                nc.tensor.transpose(u_q[i][:, h * D : (h + 1) * D], q_t[g][:, h, t * P : (t + 1) * P], ident[:])
+
+        def statistics(u, stats):
+            for h in range(0, HEADS, 2):
+                nc.vector.bn_stats(
+                    out=stats[:, h : h + 2, :].rearrange("p n k -> p (n k)"),
+                    in_=u[:, h * D : (h + 2) * D].rearrange("p (h d) -> p d h", h=2),
+                )
+
+        def inverse_deviation(s, stats, rstd):
+            nc.scalar.activation(
+                out=rstd,
+                in_=stats[:, :, 2],
                 func=ACT.Abs_reciprocal_sqrt,
                 scale=(1.0 if s == 0 else 1.0 / D),
                 bias=eps_col[:, s : s + 1],
             )
 
-        def normalise(block, first_tile):
-            g, s = divmod(block, 2)
-            for t in range(first_tile, first_tile + RUN):
-                f_sb = f_pool.tile([P, HEADS * D], F32, name="f_sb")
+        def normalise_vector(f, u, h, mean, rstd):
+            nc.vector.tensor_scalar(
+                out=f[:, h * D : (h + 1) * D],
+                in0=u[:, h * D : (h + 1) * D],
+                scalar1=mean[:, h : h + 1],
+                scalar2=rstd[:, h : h + 1],
+                op0=ALU.subtract,
+                op1=ALU.mult,
+            )
+
+        def normalise_scalar(f, u, h, rstd, shift):
+            nc.scalar.activation(
+                out=f[:, h * D : (h + 1) * D],
+                in_=u[:, h * D : (h + 1) * D],
+                func=ACT.Identity,
+                scale=rstd[:, h : h + 1],
+                bias=shift[:, h : h + 1],
+            )
+
+        def store(s, i, f):
+            g, t = divmod(i, TILES)
+            nc.sync.dma_start(out=out_dram[s][g][:, t, :], in_=f[:])
+
+        def unit(i):
+            return i if 0 <= i < N_TILES else None
+
+        fresh = []
+        waiting = range(JOBS_FIRST, len(jobs))
+        stats = rstd = None
+        for j in range(N_TILES + Q_LAG + HEADS + 2):
+            k_new, q_head, q_new = unit(j), unit(j - Q_LAG), unit(j - Q_LAG - HEADS)
+            k_mid, q_mid = unit(j - 1), unit(j - Q_LAG - HEADS - 1)
+            k_old, q_old = unit(j - 2), unit(j - Q_LAG - HEADS - 2)
+            old_stats = stats
+            rows = slice(0 if q_old is not None else HEADS, 2 * HEADS if k_old is not None else HEADS)
+            if rows.start < rows.stop:
+                rstd = small.tile([P, 2 * HEADS], F32, name="rstd")
+                shift = small.tile([P, 2 * HEADS], F32, name="shift")
+            if q_old is not None:
+                inverse_deviation(0, old_stats[:, 0:HEADS, :], rstd[:, 0:HEADS])
+            if k_old is not None:
+                inverse_deviation(1, old_stats[:, HEADS:, :], rstd[:, HEADS:])
+            if rows.start < rows.stop:
+                nc.vector.scalar_tensor_tensor(
+                    out=shift[:, rows],
+                    in0=old_stats[:, rows, 1],
+                    scalar=-1.0,
+                    in1=rstd[:, rows],
+                    op0=ALU.mult,
+                    op1=ALU.mult,
+                )
+            for n in fresh:
+                job_group(n, nc.scalar.copy)
+            if q_old is not None:
+                f_q = f_pool.tile([P, F], F32, name="f_q")
                 for h in range(HEADS):
-                    n = t * HEADS + h
-                    nc.vector.tensor_scalar(
-                        out=f_sb[:, h * D : (h + 1) * D],
-                        in0=u_rows[block, t][:, h * D : (h + 1) * D],
-                        scalar1=stats[block][:, n, 1:2],
-                        scalar2=rstd[block][:, n : n + 1],
-                        op0=ALU.subtract,
-                        op1=ALU.mult,
-                    )
-                nc.sync.dma_start(out=out_dram[s][g][:, t, :], in_=f_sb[:])
-
-        for n in range(JOBS_FIRST):
-            job_transpose(n)
-            job_group(n)
-            if n > 0:
-                job_quantise(n - 1)
-        gb_f32 = const.tile([P, P], F32)
-        nc.vector.tensor_copy(out=gb_f32[:], in_=gb_rows[:])
-        gb_bank = kt_psum.tile([P, 2, 2 * P], F32, name="kt")
-        nc.tensor.transpose(gb_bank[:, 0, 0:P], gb_f32[:], ident[:])
-        gb_col = const.tile([P, 2], F32)
-        nc.vector.tensor_copy(out=gb_col[:], in_=gb_bank[:, 0, 0:2])
-
-        def part_of_block(r):
-            if 0 <= r < N_ROUNDS:
-                return r // ROUNDS, (r % ROUNDS) * RUN
-            return None
-
-        done = JOBS_FIRST
-        quantised = JOBS_FIRST - 1
-        for j in range(N_ROUNDS + 4):
-            fresh = range(done, min(done + JOBS_PER_ROUND, len(jobs)))
-            if part_of_block(j - 4) is not None:
-                inverse_deviation(*part_of_block(j - 4))
-            if part_of_block(j) is not None:
-                project(*part_of_block(j))
-            if part_of_block(j - 2) is not None:
-                tokens_to_partitions(*part_of_block(j - 2), len(fresh) == 0)
+                    normalise_scalar(f_q, u_q[q_old], h, rstd[:, 0:HEADS], shift[:, 0:HEADS])
+                store(0, q_old, f_q)
+            if k_new is not None:
+                project_k(k_new)
+            if q_head is not None:
+                project_q(q_head)
+            if q_new is not None:
+                transpose_back_q(q_new)
+            n_jobs = JOBS_EARLY if j < EARLY_ROUNDS else 1
+            transposed, waiting = waiting[:n_jobs], waiting[n_jobs:]
+            for m, n in enumerate(transposed):
+                job_transpose(n, *job_pools[m])
+            if k_new is not None:
+                affine_k(k_new)
+            stats = small.tile([P, 2 * HEADS, 3], F32, name="stats")
+            if q_mid is not None:
+                statistics(u_q[q_mid], stats[:, 0:HEADS, :])
+            if k_mid is not None:
+                statistics(u_k[k_mid], stats[:, HEADS:, :])
             for n in fresh:
-                job_transpose(n)
-            for n in fresh:
-                if n % 2 == 1:
-                    job_group(n)
-            for n in range(quantised, done):
                 job_quantise(n)
-            quantised = done
-            done = done + len(fresh)
-            if part_of_block(j - 3) is not None:
-                statistics(*part_of_block(j - 3))
-            for n in fresh:
-                if n % 2 == 0:
-                    job_group(n)
-            if part_of_block(j - 4) is not None:
-                normalise(*part_of_block(j - 4))
+            fresh = transposed
+            if k_old is not None:
+                f_k = f_pool.tile([P, F], F32, name="f_k")
+                for h in range(HEADS):
+                    if h < K_VECTOR:
+                        normalise_vector(f_k, u_k[k_old], h, old_stats[:, HEADS:, 1], rstd[:, HEADS:])
+                    else:
+                        normalise_scalar(f_k, u_k[k_old], h, rstd[:, HEADS:], shift[:, HEADS:])
+                store(1, k_old, f_k)

@@ -24,12 +24,15 @@ WORDS = K_PASS // 2
 GROUP = 512
 N_GROUPS = TOKENS // GROUP
 TILES = GROUP // P
-N_TILES = N_GROUPS * TILES
-Q_LAG = 3
-JOBS_FIRST = 8
-EARLY_ROUNDS = 3
-JOBS_EARLY = 3
-K_VECTOR = 2
+N_BLOCKS = 2 * N_GROUPS
+ROUNDS = 2
+N_ROUNDS = ROUNDS * N_BLOCKS
+PAIR = HEADS // ROUNDS
+HALF = GROUP // 2
+MOST = 3
+JOBS_FIRST = 12
+EARLY_ROUNDS = 2
+GPSIMD_HEADS = 1
 
 FLOPS = 2 * TOKENS * HID * 2 * F
 
@@ -44,11 +47,12 @@ def tile_rebasedlinearattention_pa_t_kernel(tc, hidden_states, Wq, Wk, gamma, be
 
     with ExitStack() as stack:
         const = stack.enter_context(tc.tile_pool(name="const", bufs=1))
-        raw_pool = stack.enter_context(tc.tile_pool(name="raw", bufs=20))
+        raw_pool = stack.enter_context(tc.tile_pool(name="raw", bufs=16))
         grouped_pool = stack.enter_context(tc.tile_pool(name="grouped", bufs=6))
-        ut_pool = stack.enter_context(tc.tile_pool(name="ut", bufs=2))
-        uk_pool = stack.enter_context(tc.tile_pool(name="uk", bufs=4))
-        f_pool = stack.enter_context(tc.tile_pool(name="f", bufs=6))
+        ut_pool = stack.enter_context(tc.tile_pool(name="ut", bufs=3))
+        scaled_pool = stack.enter_context(tc.tile_pool(name="scaled", bufs=3))
+        u_pool = stack.enter_context(tc.tile_pool(name="u", bufs=12))
+        f_pool = stack.enter_context(tc.tile_pool(name="f", bufs=8))
         small = stack.enter_context(tc.tile_pool(name="small", bufs=4))
         kt_psum = stack.enter_context(tc.psum_pool(name="kt", bufs=2))
         mx_psum = stack.enter_context(tc.psum_pool(name="mx", bufs=3))
@@ -82,9 +86,9 @@ def tile_rebasedlinearattention_pa_t_kernel(tc, hidden_states, Wq, Wk, gamma, be
         load_tokens(0, 0)
         nc.sync.dma_start(out=gb_row[0:1, 0:D], in_=gamma.rearrange("(o d) -> o d", o=1))
         nc.sync.dma_start(out=gb_row[0:1, D : 2 * D], in_=beta.rearrange("(o d) -> o d", o=1))
-        load_weights(1)
-        load_tokens(0, 2)
         load_weights(0)
+        load_tokens(0, 2)
+        load_weights(1)
         for g in range(1, N_GROUPS):
             load_tokens(g, 0)
             load_tokens(g, 2)
@@ -101,6 +105,7 @@ def tile_rebasedlinearattention_pa_t_kernel(tc, hidden_states, Wq, Wk, gamma, be
 
         job_bank = {}
         job_grouped = {}
+        job_pools = ((kt_psum, "kt"), (kt_psum, "kt"), (bt_psum, "bank"))
 
         def job_transpose(n, pool, name):
             words, c, codes, scales = jobs[n]
@@ -120,179 +125,200 @@ def tile_rebasedlinearattention_pa_t_kernel(tc, hidden_states, Wq, Wk, gamma, be
                 out=codes.bitcast(FP8X4), scales=scales, in_=job_grouped[n][:].rearrange("p r t -> p (r t)")
             )
 
-        job_pools = [(kt_psum, "kt"), (kt_psum, "kt"), (bt_psum, "bank")]
+        def feature_tiles(block, half):
+            return [(block, half)] if block % 2 == 0 else [(block, 2 * half), (block, 2 * half + 1)]
+
+        def token_tiles(block, half):
+            return [(block, 2 + half)] if block % 2 == 0 else []
+
+        u = {}
+
+        u_t = {}
+        acc_t = {}
+        bank = {}
+
+        def project_features(block, half):
+            g, s = divmod(block, 2)
+            width = HALF if s == 0 else GROUP
+            if half == 0:
+                u_t[block] = ut_pool.tile([P, HEADS, width], F32, name="u_t")
+            acc_t[block, half] = []
+            for h in range(PAIR * half, PAIR * (half + 1)):
+                place = (h * width) % GROUP
+                if place == 0:
+                    acc = mx_psum.tile([P, GROUP], F32, name="acc")
+                    acc_t[block, half].append((h, acc))
+                cols = slice((s * HEADS + h) * D, (s * HEADS + h + 1) * D)
+                for c in range(PASSES):
+                    nc.tensor.matmul_mx(
+                        out=acc[:, place : place + width],
+                        lhsT=w_codes[:, c, cols].bitcast(FP8X4),
+                        lhsT_scale=w_scales[:, c, cols],
+                        rhs=x_codes[:, g, c, 0:width].bitcast(FP8X4),
+                        rhs_scale=x_scales[:, g, c, 0:width],
+                        start=(c == 0),
+                        stop=(c == PASSES - 1),
+                    )
+
+        def affine_features(block, half):
+            for h, acc in acc_t[block, half]:
+                heads = GROUP // u_t[block].shape[2]
+                nc.scalar.activation(
+                    out=u_t[block][:, h : h + heads, :].rearrange("p h n -> p (h n)"),
+                    in_=acc[:],
+                    func=ACT.Identity,
+                    scale=gb_col[:, 0:1],
+                    bias=gb_col[:, 1:2],
+                )
+
+        def transpose_back(block, t):
+            bank[block, t] = bt_psum.tile([P, F], F32, name="bank")
+            for h in range(HEADS):
+                nc.tensor.transpose(bank[block, t][:, h * D : (h + 1) * D], u_t[block][:, h, t * P : (t + 1) * P], ident[:])
+
+        def copy_back(block, t):
+            u[block, t] = u_pool.tile([P, F], F32, name="u")
+            nc.scalar.copy(out=u[block, t][:], in_=bank[block, t][:])
+
+        acc_k = {}
+
+        def project_tokens(block, t):
+            g, s = divmod(block, 2)
+            rows = slice(t * P, (t + 1) * P)
+            cols = slice(s * F, (s + 1) * F)
+            acc_k[block, t] = mx_psum.tile([P, F], F32, name="acc")
+            for c in range(PASSES):
+                nc.tensor.matmul_mx(
+                    out=acc_k[block, t][:],
+                    lhsT=x_codes[:, g, c, rows].bitcast(FP8X4),
+                    lhsT_scale=x_scales[:, g, c, rows],
+                    rhs=w_codes[:, c, cols].bitcast(FP8X4),
+                    rhs_scale=w_scales[:, c, cols],
+                    start=(c == 0),
+                    stop=(c == PASSES - 1),
+                )
+
+        def by_head(tile):
+            return tile[:].rearrange("p (h d) -> p h d", h=HEADS)
+
+        def affine_tokens(block, t):
+            scaled = scaled_pool.tile([P, F], F32, name="scaled")
+            nc.vector.tensor_mul(out=by_head(scaled), in0=by_head(acc_k[block, t]), in1=gamma_all)
+            u[block, t] = u_pool.tile([P, F], F32, name="u")
+            nc.gpsimd.tensor_add(out=by_head(u[block, t]), in0=by_head(scaled), in1=beta_all)
+
+        def statistics(tiles, stats):
+            for i, tile in enumerate(tiles):
+                for h in range(0, HEADS, 2):
+                    n = i * HEADS + h
+                    nc.vector.bn_stats(
+                        out=stats[:, n : n + 2, :].rearrange("p n k -> p (n k)"),
+                        in_=u[tile][:, h * D : (h + 2) * D].rearrange("p (h d) -> p d h", h=2),
+                    )
+
+        def inverse_deviation(tiles, stats, rstd, minus_mean):
+            rows = slice(0, len(tiles) * HEADS)
+            nc.scalar.mul(out=minus_mean[:, rows], in_=stats[:, rows, 1], mul=-1.0)
+            for s in range(2):
+                places = [i for i, tile in enumerate(tiles) if tile[0] % 2 == s]
+                if places:
+                    rows = slice(places[0] * HEADS, (places[-1] + 1) * HEADS)
+                    nc.scalar.activation(
+                        out=rstd[:, rows],
+                        in_=stats[:, rows, 2],
+                        func=ACT.Abs_reciprocal_sqrt,
+                        scale=(1.0 if s == 0 else 1.0 / D),
+                        bias=eps_col[:, s : s + 1],
+                    )
+
+        def normalise(tiles, stats, rstd, minus_mean):
+            rows = slice(0, len(tiles) * HEADS)
+            shift = small.tile([P, MOST * HEADS], F32, name="shift")
+            nc.gpsimd.tensor_mul(out=shift[:, rows], in0=minus_mean[:, rows], in1=rstd[:, rows])
+            for i, (block, t) in enumerate(tiles):
+                g, s = divmod(block, 2)
+                f = f_pool.tile([P, F], F32, name="f")
+                for h in range(HEADS):
+                    n = i * HEADS + h
+                    cols = slice(h * D, (h + 1) * D)
+                    if h < HEADS - GPSIMD_HEADS:
+                        nc.vector.tensor_scalar(
+                            out=f[:, cols],
+                            in0=u[block, t][:, cols],
+                            scalar1=stats[:, n, 1:2],
+                            scalar2=rstd[:, n : n + 1],
+                            op0=ALU.subtract,
+                            op1=ALU.mult,
+                        )
+                    else:
+                        nc.gpsimd.tensor_scalar(
+                            out=f[:, cols],
+                            in0=u[block, t][:, cols],
+                            scalar1=rstd[:, n : n + 1],
+                            scalar2=shift[:, n : n + 1],
+                            op0=ALU.mult,
+                            op1=ALU.add,
+                        )
+                nc.sync.dma_start(out=out_dram[s][g][:, t, :], in_=f[:])
+
+        gb_all = const.tile([P, 2, D], F32)
+        gb_col = const.tile([P, 2], F32)
+        gamma_all, beta_all = (gb_all[:, v, :].unsqueeze(1).to_broadcast([P, HEADS, D]) for v in range(2))
         for n in range(JOBS_FIRST):
             job_transpose(n, *job_pools[n % 3])
             job_group(n, nc.vector.tensor_copy if n % 2 == 0 else nc.scalar.copy)
             if n > 0:
                 job_quantise(n - 1)
+            if n == 1:
+                gb_bank = mx_psum.tile([P, GROUP], F32, name="acc")
+                nc.tensor.matmul(out=gb_bank[:, 0 : 2 * D], lhsT=ones[:], rhs=gb_row[:], start=True, stop=True)
+                nc.scalar.copy(out=gb_all[:].rearrange("p v d -> p (v d)"), in_=gb_bank[:, 0 : 2 * D])
+            if n == 5:
+                col_bank = mx_psum.tile([P, GROUP], F32, name="acc")
+                for v in range(2):
+                    nc.tensor.transpose(col_bank[:, v * P : (v + 1) * P], gb_all[:, v, :], ident[:])
+                    nc.scalar.copy(out=gb_col[:, v : v + 1], in_=col_bank[:, v * P : v * P + 1])
         job_quantise(JOBS_FIRST - 1)
-        gb_bank = bt_psum.tile([P, F], F32, name="bank")
-        nc.tensor.matmul(out=gb_bank[:, 0 : 2 * D], lhsT=ones[:], rhs=gb_row[:], start=True, stop=True)
-        gamma_all = const.tile([P, HEADS, D], F32)
-        beta_all = const.tile([P, HEADS, D], F32)
-        for h in range(HEADS):
-            nc.scalar.copy(out=gamma_all[:, h, :], in_=gb_bank[:, 0:D])
-            nc.scalar.copy(out=beta_all[:, h, :], in_=gb_bank[:, D : 2 * D])
-        col_bank = bt_psum.tile([P, F], F32, name="bank")
-        nc.tensor.transpose(col_bank[:, 0:P], gamma_all[:, 0, :], ident[:])
-        nc.tensor.transpose(col_bank[:, P : 2 * P], beta_all[:, 0, :], ident[:])
-        gb_col = const.tile([P, 2], F32)
-        nc.scalar.copy(out=gb_col[:, 0:1], in_=col_bank[:, 0:1])
-        nc.scalar.copy(out=gb_col[:, 1:2], in_=col_bank[:, P : P + 1])
 
-        k_acc = {}
-        u_k = {}
+        def part_of_block(r):
+            return [divmod(r, ROUNDS)] if 0 <= r < N_ROUNDS else []
 
-        def project_k(i):
-            g, t = divmod(i, TILES)
-            rows = slice(t * P, (t + 1) * P)
-            k_acc[i] = mx_psum.tile([P, F], F32, name="acc")
-            for c in range(PASSES):
-                nc.tensor.matmul_mx(
-                    out=k_acc[i][:],
-                    lhsT=x_codes[:, g, c, rows].bitcast(FP8X4),
-                    lhsT_scale=x_scales[:, g, c, rows],
-                    rhs=w_codes[:, c, F : 2 * F].bitcast(FP8X4),
-                    rhs_scale=w_scales[:, c, F : 2 * F],
-                    start=(c == 0),
-                    stop=(c == PASSES - 1),
-                )
-
-        def affine_k(i):
-            scaled = uk_pool.tile([P, F], F32, name="scaled")
-            nc.vector.tensor_mul(out=scaled[:], in0=k_acc[i][:], in1=gamma_all[:].rearrange("p h d -> p (h d)"))
-            u_k[i] = uk_pool.tile([P, F], F32, name="u_k")
-            nc.gpsimd.tensor_add(out=u_k[i][:], in0=scaled[:], in1=beta_all[:].rearrange("p h d -> p (h d)"))
-
-        q_t = {}
-        u_q = {}
-
-        def project_q(i):
-            g, h = divmod(i, HEADS)
-            if h == 0:
-                q_t[g] = ut_pool.tile([P, HEADS, GROUP], F32, name="q_t")
-            cols = slice(h * D, (h + 1) * D)
-            acc = mx_psum.tile([P, GROUP], F32, name="acc")
-            for c in range(PASSES):
-                nc.tensor.matmul_mx(
-                    out=acc[:],
-                    lhsT=w_codes[:, c, cols].bitcast(FP8X4),
-                    lhsT_scale=w_scales[:, c, cols],
-                    rhs=x_codes[:, g, c, :].bitcast(FP8X4),
-                    rhs_scale=x_scales[:, g, c, :],
-                    start=(c == 0),
-                    stop=(c == PASSES - 1),
-                )
-            nc.scalar.activation(
-                out=q_t[g][:, h, :], in_=acc[:], func=ACT.Identity, scale=gb_col[:, 0:1], bias=gb_col[:, 1:2]
-            )
-
-        def transpose_back_q(i):
-            g, t = divmod(i, TILES)
-            u_q[i] = bt_psum.tile([P, F], F32, name="bank")
-            for h in range(HEADS):
-                nc.tensor.transpose(u_q[i][:, h * D : (h + 1) * D], q_t[g][:, h, t * P : (t + 1) * P], ident[:])
-
-        def statistics(u, stats):
-            for h in range(0, HEADS, 2):
-                nc.vector.bn_stats(
-                    out=stats[:, h : h + 2, :].rearrange("p n k -> p (n k)"),
-                    in_=u[:, h * D : (h + 2) * D].rearrange("p (h d) -> p d h", h=2),
-                )
-
-        def inverse_deviation(s, stats, rstd):
-            nc.scalar.activation(
-                out=rstd,
-                in_=stats[:, :, 2],
-                func=ACT.Abs_reciprocal_sqrt,
-                scale=(1.0 if s == 0 else 1.0 / D),
-                bias=eps_col[:, s : s + 1],
-            )
-
-        def normalise_vector(f, u, h, mean, rstd):
-            nc.vector.tensor_scalar(
-                out=f[:, h * D : (h + 1) * D],
-                in0=u[:, h * D : (h + 1) * D],
-                scalar1=mean[:, h : h + 1],
-                scalar2=rstd[:, h : h + 1],
-                op0=ALU.subtract,
-                op1=ALU.mult,
-            )
-
-        def normalise_scalar(f, u, h, rstd, shift):
-            nc.scalar.activation(
-                out=f[:, h * D : (h + 1) * D],
-                in_=u[:, h * D : (h + 1) * D],
-                func=ACT.Identity,
-                scale=rstd[:, h : h + 1],
-                bias=shift[:, h : h + 1],
-            )
-
-        def store(s, i, f):
-            g, t = divmod(i, TILES)
-            nc.sync.dma_start(out=out_dram[s][g][:, t, :], in_=f[:])
-
-        def unit(i):
-            return i if 0 <= i < N_TILES else None
-
-        fresh = []
         waiting = range(JOBS_FIRST, len(jobs))
-        stats = rstd = None
-        for j in range(N_TILES + Q_LAG + HEADS + 2):
-            k_new, q_head, q_new = unit(j), unit(j - Q_LAG), unit(j - Q_LAG - HEADS)
-            k_mid, q_mid = unit(j - 1), unit(j - Q_LAG - HEADS - 1)
-            k_old, q_old = unit(j - 2), unit(j - Q_LAG - HEADS - 2)
-            old_stats = stats
-            rows = slice(0 if q_old is not None else HEADS, 2 * HEADS if k_old is not None else HEADS)
-            if rows.start < rows.stop:
-                rstd = small.tile([P, 2 * HEADS], F32, name="rstd")
-                shift = small.tile([P, 2 * HEADS], F32, name="shift")
-            if q_old is not None:
-                inverse_deviation(0, old_stats[:, 0:HEADS, :], rstd[:, 0:HEADS])
-            if k_old is not None:
-                inverse_deviation(1, old_stats[:, HEADS:, :], rstd[:, HEADS:])
-            if rows.start < rows.stop:
-                nc.vector.scalar_tensor_tensor(
-                    out=shift[:, rows],
-                    in0=old_stats[:, rows, 1],
-                    scalar=-1.0,
-                    in1=rstd[:, rows],
-                    op0=ALU.mult,
-                    op1=ALU.mult,
-                )
-            for n in fresh:
-                job_group(n, nc.scalar.copy)
-            if q_old is not None:
-                f_q = f_pool.tile([P, F], F32, name="f_q")
-                for h in range(HEADS):
-                    normalise_scalar(f_q, u_q[q_old], h, rstd[:, 0:HEADS], shift[:, 0:HEADS])
-                store(0, q_old, f_q)
-            if k_new is not None:
-                project_k(k_new)
-            if q_head is not None:
-                project_q(q_head)
-            if q_new is not None:
-                transpose_back_q(q_new)
-            n_jobs = JOBS_EARLY if j < EARLY_ROUNDS else 1
+        fresh = []
+        counted = ()
+        for r in range(N_ROUNDS + 5):
+            n_jobs = 2 if r < EARLY_ROUNDS else 1
             transposed, waiting = waiting[:n_jobs], waiting[n_jobs:]
-            for m, n in enumerate(transposed):
-                job_transpose(n, *job_pools[m])
-            if k_new is not None:
-                affine_k(k_new)
-            stats = small.tile([P, 2 * HEADS, 3], F32, name="stats")
-            if q_mid is not None:
-                statistics(u_q[q_mid], stats[:, 0:HEADS, :])
-            if k_mid is not None:
-                statistics(u_k[k_mid], stats[:, HEADS:, :])
+            new = part_of_block(r)
+            back = [tile for part in part_of_block(r - 2) for tile in feature_tiles(*part)]
+            tiles = [tile for part in part_of_block(r - 3) for tile in feature_tiles(*part)]
+            tiles += [tile for part in part_of_block(r - 1) for tile in token_tiles(*part)]
+            for part in new:
+                project_features(*part)
+                for tile in token_tiles(*part):
+                    project_tokens(*tile)
+            for tile in back:
+                transpose_back(*tile)
+            for i, n in enumerate(transposed):
+                job_transpose(n, *job_pools[i])
+            for part in new:
+                for tile in token_tiles(*part):
+                    affine_tokens(*tile)
+            stats = small.tile([P, MOST * HEADS, 3], F32, name="stats")
+            statistics(tiles, stats)
+            for part in new:
+                affine_features(*part)
+            if counted:
+                rstd = small.tile([P, MOST * HEADS], F32, name="rstd")
+                minus_mean = small.tile([P, MOST * HEADS], F32, name="minus_mean")
+                inverse_deviation(*counted, rstd, minus_mean)
             for n in fresh:
                 job_quantise(n)
+            for tile in back:
+                copy_back(*tile)
+            for n in transposed:
+                job_group(n, nc.scalar.copy)
+            if counted:
+                normalise(*counted, rstd, minus_mean)
             fresh = transposed
-            if k_old is not None:
-                f_k = f_pool.tile([P, F], F32, name="f_k")
-                for h in range(HEADS):
-                    if h < K_VECTOR:
-                        normalise_vector(f_k, u_k[k_old], h, old_stats[:, HEADS:, 1], rstd[:, HEADS:])
-                    else:
-                        normalise_scalar(f_k, u_k[k_old], h, rstd[:, HEADS:], shift[:, HEADS:])
-                store(1, k_old, f_k)
+            counted = (tiles, stats) if tiles else ()

@@ -29,10 +29,9 @@ ROUNDS = 2
 N_ROUNDS = ROUNDS * N_BLOCKS
 PAIR = HEADS // ROUNDS
 HALF = GROUP // 2
-MOST = 3
+RUN = TILES // ROUNDS
 JOBS_FIRST = 12
 EARLY_ROUNDS = 2
-GPSIMD_HEADS = 1
 
 FLOPS = 2 * TOKENS * HID * 2 * F
 
@@ -55,8 +54,8 @@ def tile_rebasedlinearattention_pa_t_kernel(tc, hidden_states, Wq, Wk, gamma, be
         f_pool = stack.enter_context(tc.tile_pool(name="f", bufs=8))
         small = stack.enter_context(tc.tile_pool(name="small", bufs=4))
         kt_psum = stack.enter_context(tc.psum_pool(name="kt", bufs=2))
-        mx_psum = stack.enter_context(tc.psum_pool(name="mx", bufs=3))
-        bt_psum = stack.enter_context(tc.psum_pool(name="bt", bufs=3))
+        mx_psum = stack.enter_context(tc.psum_pool(name="mx", bufs=2))
+        bt_psum = stack.enter_context(tc.psum_pool(name="bt", bufs=4))
         stack.enter_context(tc.manual_schedule())
 
         w_codes = const.tile([P, PASSES, 2 * F], U32, align_bytes=64)
@@ -131,6 +130,9 @@ def tile_rebasedlinearattention_pa_t_kernel(tc, hidden_states, Wq, Wk, gamma, be
         def token_tiles(block, half):
             return [(block, 2 + half)] if block % 2 == 0 else []
 
+        def stays(block, t):
+            return block % 2 == 1 and t == TILES - 1
+
         u = {}
 
         u_t = {}
@@ -177,6 +179,9 @@ def tile_rebasedlinearattention_pa_t_kernel(tc, hidden_states, Wq, Wk, gamma, be
                 nc.tensor.transpose(bank[block, t][:, h * D : (h + 1) * D], u_t[block][:, h, t * P : (t + 1) * P], ident[:])
 
         def copy_back(block, t):
+            if stays(block, t):
+                u[block, t] = bank[block, t]
+                return
             u[block, t] = u_pool.tile([P, F], F32, name="u")
             nc.scalar.copy(out=u[block, t][:], in_=bank[block, t][:])
 
@@ -216,32 +221,37 @@ def tile_rebasedlinearattention_pa_t_kernel(tc, hidden_states, Wq, Wk, gamma, be
                         in_=u[tile][:, h * D : (h + 2) * D].rearrange("p (h d) -> p d h", h=2),
                     )
 
-        def inverse_deviation(tiles, stats, rstd, minus_mean):
-            rows = slice(0, len(tiles) * HEADS)
-            nc.scalar.mul(out=minus_mean[:, rows], in_=stats[:, rows, 1], mul=-1.0)
-            for s in range(2):
-                places = [i for i, tile in enumerate(tiles) if tile[0] % 2 == s]
-                if places:
-                    rows = slice(places[0] * HEADS, (places[-1] + 1) * HEADS)
-                    nc.scalar.activation(
-                        out=rstd[:, rows],
-                        in_=stats[:, rows, 2],
-                        func=ACT.Abs_reciprocal_sqrt,
-                        scale=(1.0 if s == 0 else 1.0 / D),
-                        bias=eps_col[:, s : s + 1],
-                    )
+        def inverse_deviation(tiles, stats, rstd):
+            s = tiles[0][0] % 2
+            nc.scalar.activation(
+                out=rstd[:],
+                in_=stats[:, :, 2],
+                func=ACT.Abs_reciprocal_sqrt,
+                scale=(1.0 if s == 0 else 1.0 / D),
+                bias=eps_col[:, s : s + 1],
+            )
 
-        def normalise(tiles, stats, rstd, minus_mean):
-            rows = slice(0, len(tiles) * HEADS)
-            shift = small.tile([P, MOST * HEADS], F32, name="shift")
-            nc.gpsimd.tensor_mul(out=shift[:, rows], in0=minus_mean[:, rows], in1=rstd[:, rows])
+        def normalise(tiles, stats, rstd):
+            if any(stays(*tile) for tile in tiles):
+                shift = small.tile([P, RUN * HEADS], F32, name="shift")
+                nc.vector.scalar_tensor_tensor(
+                    out=shift[:], in0=stats[:, :, 1], scalar=-1.0, in1=rstd[:], op0=ALU.mult, op1=ALU.mult
+                )
             for i, (block, t) in enumerate(tiles):
                 g, s = divmod(block, 2)
                 f = f_pool.tile([P, F], F32, name="f")
                 for h in range(HEADS):
                     n = i * HEADS + h
                     cols = slice(h * D, (h + 1) * D)
-                    if h < HEADS - GPSIMD_HEADS:
+                    if stays(block, t):
+                        nc.scalar.activation(
+                            out=f[:, cols],
+                            in_=u[block, t][:, cols],
+                            func=ACT.Identity,
+                            scale=rstd[:, n : n + 1],
+                            bias=shift[:, n : n + 1],
+                        )
+                    else:
                         nc.vector.tensor_scalar(
                             out=f[:, cols],
                             in0=u[block, t][:, cols],
@@ -249,15 +259,6 @@ def tile_rebasedlinearattention_pa_t_kernel(tc, hidden_states, Wq, Wk, gamma, be
                             scalar2=rstd[:, n : n + 1],
                             op0=ALU.subtract,
                             op1=ALU.mult,
-                        )
-                    else:
-                        nc.gpsimd.tensor_scalar(
-                            out=f[:, cols],
-                            in0=u[block, t][:, cols],
-                            scalar1=rstd[:, n : n + 1],
-                            scalar2=shift[:, n : n + 1],
-                            op0=ALU.mult,
-                            op1=ALU.add,
                         )
                 nc.sync.dma_start(out=out_dram[s][g][:, t, :], in_=f[:])
 
@@ -273,7 +274,7 @@ def tile_rebasedlinearattention_pa_t_kernel(tc, hidden_states, Wq, Wk, gamma, be
                 gb_bank = mx_psum.tile([P, GROUP], F32, name="acc")
                 nc.tensor.matmul(out=gb_bank[:, 0 : 2 * D], lhsT=ones[:], rhs=gb_row[:], start=True, stop=True)
                 nc.scalar.copy(out=gb_all[:].rearrange("p v d -> p (v d)"), in_=gb_bank[:, 0 : 2 * D])
-            if n == 5:
+            if n == 8:
                 col_bank = mx_psum.tile([P, GROUP], F32, name="acc")
                 for v in range(2):
                     nc.tensor.transpose(col_bank[:, v * P : (v + 1) * P], gb_all[:, v, :], ident[:])
@@ -290,35 +291,34 @@ def tile_rebasedlinearattention_pa_t_kernel(tc, hidden_states, Wq, Wk, gamma, be
             n_jobs = 2 if r < EARLY_ROUNDS else 1
             transposed, waiting = waiting[:n_jobs], waiting[n_jobs:]
             new = part_of_block(r)
+            new_tokens = [tile for part in new for tile in token_tiles(*part)]
             back = [tile for part in part_of_block(r - 2) for tile in feature_tiles(*part)]
-            tiles = [tile for part in part_of_block(r - 3) for tile in feature_tiles(*part)]
-            tiles += [tile for part in part_of_block(r - 1) for tile in token_tiles(*part)]
+            tiles = [tile for part in part_of_block(r - 3) for tile in feature_tiles(*part) + token_tiles(*part)]
+            for tile in new_tokens:
+                project_tokens(*tile)
             for part in new:
                 project_features(*part)
-                for tile in token_tiles(*part):
-                    project_tokens(*tile)
             for tile in back:
                 transpose_back(*tile)
             for i, n in enumerate(transposed):
                 job_transpose(n, *job_pools[i])
-            for part in new:
-                for tile in token_tiles(*part):
-                    affine_tokens(*tile)
-            stats = small.tile([P, MOST * HEADS, 3], F32, name="stats")
-            statistics(tiles, stats)
+            for tile in new_tokens:
+                affine_tokens(*tile)
+            for n in fresh:
+                job_quantise(n)
+            fresh = transposed
+            if tiles:
+                stats = small.tile([P, RUN * HEADS, 3], F32, name="stats")
+                statistics(tiles, stats)
             for part in new:
                 affine_features(*part)
             if counted:
-                rstd = small.tile([P, MOST * HEADS], F32, name="rstd")
-                minus_mean = small.tile([P, MOST * HEADS], F32, name="minus_mean")
-                inverse_deviation(*counted, rstd, minus_mean)
-            for n in fresh:
-                job_quantise(n)
+                rstd = small.tile([P, RUN * HEADS], F32, name="rstd")
+                inverse_deviation(*counted, rstd)
             for tile in back:
                 copy_back(*tile)
             for n in transposed:
                 job_group(n, nc.scalar.copy)
             if counted:
-                normalise(*counted, rstd, minus_mean)
-            fresh = transposed
+                normalise(*counted, rstd)
             counted = (tiles, stats) if tiles else ()

@@ -30,6 +30,7 @@ N_ROUNDS = ROUNDS * N_BLOCKS
 PAIR = HEADS // ROUNDS
 HALF = GROUP // 2
 RUN = TILES // ROUNDS
+K_VECTOR = HEADS // 2
 JOBS_FIRST = 12
 EARLY_ROUNDS = 2
 
@@ -50,9 +51,9 @@ def tile_rebasedlinearattention_pa_t_kernel(tc, hidden_states, Wq, Wk, gamma, be
         grouped_pool = stack.enter_context(tc.tile_pool(name="grouped", bufs=6))
         ut_pool = stack.enter_context(tc.tile_pool(name="ut", bufs=3))
         scaled_pool = stack.enter_context(tc.tile_pool(name="scaled", bufs=3))
-        u_pool = stack.enter_context(tc.tile_pool(name="u", bufs=12))
+        u_pool = stack.enter_context(tc.tile_pool(name="u", bufs=8))
         f_pool = stack.enter_context(tc.tile_pool(name="f", bufs=8))
-        small = stack.enter_context(tc.tile_pool(name="small", bufs=4))
+        small = stack.enter_context(tc.tile_pool(name="small", bufs=6))
         kt_psum = stack.enter_context(tc.psum_pool(name="kt", bufs=2))
         mx_psum = stack.enter_context(tc.psum_pool(name="mx", bufs=2))
         bt_psum = stack.enter_context(tc.psum_pool(name="bt", bufs=4))
@@ -124,77 +125,54 @@ def tile_rebasedlinearattention_pa_t_kernel(tc, hidden_states, Wq, Wk, gamma, be
                 out=codes.bitcast(FP8X4), scales=scales, in_=job_grouped[n][:].rearrange("p r t -> p (r t)")
             )
 
-        def feature_tiles(block, half):
-            return [(block, half)] if block % 2 == 0 else [(block, 2 * half), (block, 2 * half + 1)]
-
-        def token_tiles(block, half):
-            return [(block, 2 + half)] if block % 2 == 0 else []
-
-        def stays(block, t):
-            return block % 2 == 1 and t == TILES - 1
-
         u = {}
 
         u_t = {}
-        acc_t = {}
-        bank = {}
+        acc_f = {}
 
         def project_features(block, half):
             g, s = divmod(block, 2)
-            width = HALF if s == 0 else GROUP
-            if half == 0:
-                u_t[block] = ut_pool.tile([P, HEADS, width], F32, name="u_t")
-            acc_t[block, half] = []
-            for h in range(PAIR * half, PAIR * (half + 1)):
-                place = (h * width) % GROUP
-                if place == 0:
-                    acc = mx_psum.tile([P, GROUP], F32, name="acc")
-                    acc_t[block, half].append((h, acc))
-                cols = slice((s * HEADS + h) * D, (s * HEADS + h + 1) * D)
+            acc_f[block, half] = mx_psum.tile([P, PAIR, HALF], F32, name="acc")
+            for i in range(PAIR):
+                head = s * HEADS + PAIR * half + i
+                cols = slice(head * D, (head + 1) * D)
                 for c in range(PASSES):
                     nc.tensor.matmul_mx(
-                        out=acc[:, place : place + width],
+                        out=acc_f[block, half][:, i, :],
                         lhsT=w_codes[:, c, cols].bitcast(FP8X4),
                         lhsT_scale=w_scales[:, c, cols],
-                        rhs=x_codes[:, g, c, 0:width].bitcast(FP8X4),
-                        rhs_scale=x_scales[:, g, c, 0:width],
+                        rhs=x_codes[:, g, c, 0:HALF].bitcast(FP8X4),
+                        rhs_scale=x_scales[:, g, c, 0:HALF],
                         start=(c == 0),
                         stop=(c == PASSES - 1),
                     )
 
         def affine_features(block, half):
-            for h, acc in acc_t[block, half]:
-                heads = GROUP // u_t[block].shape[2]
-                nc.scalar.activation(
-                    out=u_t[block][:, h : h + heads, :].rearrange("p h n -> p (h n)"),
-                    in_=acc[:],
-                    func=ACT.Identity,
-                    scale=gb_col[:, 0:1],
-                    bias=gb_col[:, 1:2],
-                )
+            if half == 0:
+                u_t[block] = ut_pool.tile([P, HEADS, HALF], F32, name="u_t")
+            nc.scalar.activation(
+                out=u_t[block][:, PAIR * half : PAIR * (half + 1), :],
+                in_=acc_f[block, half][:],
+                func=ACT.Identity,
+                scale=gb_col[:, 0:1],
+                bias=gb_col[:, 1:2],
+            )
 
         def transpose_back(block, t):
-            bank[block, t] = bt_psum.tile([P, F], F32, name="bank")
+            u[block, t] = bt_psum.tile([P, F], F32, name="bank")
             for h in range(HEADS):
-                nc.tensor.transpose(bank[block, t][:, h * D : (h + 1) * D], u_t[block][:, h, t * P : (t + 1) * P], ident[:])
+                nc.tensor.transpose(u[block, t][:, h * D : (h + 1) * D], u_t[block][:, h, t * P : (t + 1) * P], ident[:])
 
-        def copy_back(block, t):
-            if stays(block, t):
-                u[block, t] = bank[block, t]
-                return
-            u[block, t] = u_pool.tile([P, F], F32, name="u")
-            nc.scalar.copy(out=u[block, t][:], in_=bank[block, t][:])
-
-        acc_k = {}
+        acc_t = {}
 
         def project_tokens(block, t):
             g, s = divmod(block, 2)
             rows = slice(t * P, (t + 1) * P)
             cols = slice(s * F, (s + 1) * F)
-            acc_k[block, t] = mx_psum.tile([P, F], F32, name="acc")
+            acc_t[block, t] = mx_psum.tile([P, F], F32, name="acc")
             for c in range(PASSES):
                 nc.tensor.matmul_mx(
-                    out=acc_k[block, t][:],
+                    out=acc_t[block, t][:],
                     lhsT=x_codes[:, g, c, rows].bitcast(FP8X4),
                     lhsT_scale=x_scales[:, g, c, rows],
                     rhs=w_codes[:, c, cols].bitcast(FP8X4),
@@ -208,59 +186,71 @@ def tile_rebasedlinearattention_pa_t_kernel(tc, hidden_states, Wq, Wk, gamma, be
 
         def affine_tokens(block, t):
             scaled = scaled_pool.tile([P, F], F32, name="scaled")
-            nc.vector.tensor_mul(out=by_head(scaled), in0=by_head(acc_k[block, t]), in1=gamma_all)
+            nc.vector.tensor_mul(out=by_head(scaled), in0=by_head(acc_t[block, t]), in1=gamma_all)
             u[block, t] = u_pool.tile([P, F], F32, name="u")
             nc.gpsimd.tensor_add(out=by_head(u[block, t]), in0=by_head(scaled), in1=beta_all)
 
-        def statistics(tiles, stats):
-            for i, tile in enumerate(tiles):
+        stats = {}
+        rstd = {}
+        shift = {}
+
+        def tiles_of(block, half):
+            return [(block, half), (block, 2 + half)]
+
+        def statistics(part):
+            stats[part] = small.tile([P, RUN * HEADS, 3], F32, name="stats")
+            for i, tile in enumerate(tiles_of(*part)):
                 for h in range(0, HEADS, 2):
                     n = i * HEADS + h
                     nc.vector.bn_stats(
-                        out=stats[:, n : n + 2, :].rearrange("p n k -> p (n k)"),
+                        out=stats[part][:, n : n + 2, :].rearrange("p n k -> p (n k)"),
                         in_=u[tile][:, h * D : (h + 2) * D].rearrange("p (h d) -> p d h", h=2),
                     )
 
-        def inverse_deviation(tiles, stats, rstd):
-            s = tiles[0][0] % 2
+        def inverse_deviation(part):
+            s = part[0] % 2
+            rstd[part] = small.tile([P, RUN * HEADS], F32, name="rstd")
             nc.scalar.activation(
-                out=rstd[:],
-                in_=stats[:, :, 2],
+                out=rstd[part][:],
+                in_=stats[part][:, :, 2],
                 func=ACT.Abs_reciprocal_sqrt,
                 scale=(1.0 if s == 0 else 1.0 / D),
                 bias=eps_col[:, s : s + 1],
             )
 
-        def normalise(tiles, stats, rstd):
-            if any(stays(*tile) for tile in tiles):
-                shift = small.tile([P, RUN * HEADS], F32, name="shift")
-                nc.vector.scalar_tensor_tensor(
-                    out=shift[:], in0=stats[:, :, 1], scalar=-1.0, in1=rstd[:], op0=ALU.mult, op1=ALU.mult
+        def minus_mean_rstd(part):
+            shift[part] = small.tile([P, RUN * HEADS], F32, name="shift")
+            nc.vector.scalar_tensor_tensor(
+                out=shift[part][:], in0=stats[part][:, :, 1], scalar=-1.0, in1=rstd[part][:], op0=ALU.mult, op1=ALU.mult
+            )
+
+        def normalise_scalar(part, i, f, heads):
+            for h in heads:
+                n = i * HEADS + h
+                nc.scalar.activation(
+                    out=f[:, h * D : (h + 1) * D],
+                    in_=u[tiles_of(*part)[i]][:, h * D : (h + 1) * D],
+                    func=ACT.Identity,
+                    scale=rstd[part][:, n : n + 1],
+                    bias=shift[part][:, n : n + 1],
                 )
-            for i, (block, t) in enumerate(tiles):
-                g, s = divmod(block, 2)
-                f = f_pool.tile([P, F], F32, name="f")
-                for h in range(HEADS):
-                    n = i * HEADS + h
-                    cols = slice(h * D, (h + 1) * D)
-                    if stays(block, t):
-                        nc.scalar.activation(
-                            out=f[:, cols],
-                            in_=u[block, t][:, cols],
-                            func=ACT.Identity,
-                            scale=rstd[:, n : n + 1],
-                            bias=shift[:, n : n + 1],
-                        )
-                    else:
-                        nc.vector.tensor_scalar(
-                            out=f[:, cols],
-                            in0=u[block, t][:, cols],
-                            scalar1=stats[:, n, 1:2],
-                            scalar2=rstd[:, n : n + 1],
-                            op0=ALU.subtract,
-                            op1=ALU.mult,
-                        )
-                nc.sync.dma_start(out=out_dram[s][g][:, t, :], in_=f[:])
+
+        def normalise_vector(part, i, f, heads):
+            for h in heads:
+                n = i * HEADS + h
+                nc.vector.tensor_scalar(
+                    out=f[:, h * D : (h + 1) * D],
+                    in0=u[tiles_of(*part)[i]][:, h * D : (h + 1) * D],
+                    scalar1=stats[part][:, n, 1:2],
+                    scalar2=rstd[part][:, n : n + 1],
+                    op0=ALU.subtract,
+                    op1=ALU.mult,
+                )
+
+        def store(part, i, f):
+            block, t = tiles_of(*part)[i]
+            g, s = divmod(block, 2)
+            nc.sync.dma_start(out=out_dram[s][g][:, t, :], in_=f[:])
 
         gb_all = const.tile([P, 2, D], F32)
         gb_col = const.tile([P, 2], F32)
@@ -286,39 +276,37 @@ def tile_rebasedlinearattention_pa_t_kernel(tc, hidden_states, Wq, Wk, gamma, be
 
         waiting = range(JOBS_FIRST, len(jobs))
         fresh = []
-        counted = ()
         for r in range(N_ROUNDS + 5):
             n_jobs = 2 if r < EARLY_ROUNDS else 1
             transposed, waiting = waiting[:n_jobs], waiting[n_jobs:]
-            new = part_of_block(r)
-            new_tokens = [tile for part in new for tile in token_tiles(*part)]
-            back = [tile for part in part_of_block(r - 2) for tile in feature_tiles(*part)]
-            tiles = [tile for part in part_of_block(r - 3) for tile in feature_tiles(*part) + token_tiles(*part)]
-            for tile in new_tokens:
-                project_tokens(*tile)
-            for part in new:
-                project_features(*part)
-            for tile in back:
-                transpose_back(*tile)
+            new, back, counted, inverted, last = (part_of_block(r - lag) for lag in (0, 2, 3, 4, 5))
+            for block, half in new:
+                project_tokens(block, 2 + half)
+                project_features(block, half)
+            for block, half in back:
+                transpose_back(block, half)
             for i, n in enumerate(transposed):
                 job_transpose(n, *job_pools[i])
-            for tile in new_tokens:
-                affine_tokens(*tile)
+            for part in last:
+                minus_mean_rstd(part)
+            for block, half in new:
+                affine_tokens(block, 2 + half)
             for n in fresh:
                 job_quantise(n)
             fresh = transposed
-            if tiles:
-                stats = small.tile([P, RUN * HEADS, 3], F32, name="stats")
-                statistics(tiles, stats)
+            for part in counted:
+                statistics(part)
+            for part in inverted:
+                inverse_deviation(part)
             for part in new:
                 affine_features(*part)
-            if counted:
-                rstd = small.tile([P, RUN * HEADS], F32, name="rstd")
-                inverse_deviation(*counted, rstd)
-            for tile in back:
-                copy_back(*tile)
+            f_of = [f_pool.tile([P, F], F32, name="f") for i in range(RUN * len(last))]
+            for part in last:
+                normalise_scalar(part, 0, f_of[0], range(HEADS))
+                store(part, 0, f_of[0])
             for n in transposed:
                 job_group(n, nc.scalar.copy)
-            if counted:
-                normalise(*counted, rstd)
-            counted = (tiles, stats) if tiles else ()
+            for part in last:
+                normalise_vector(part, 1, f_of[1], range(K_VECTOR))
+                normalise_scalar(part, 1, f_of[1], range(K_VECTOR, HEADS))
+                store(part, 1, f_of[1])

@@ -29,10 +29,8 @@ ROUNDS = 2
 N_ROUNDS = ROUNDS * N_BLOCKS
 PAIR = HEADS // ROUNDS
 HALF = GROUP // 2
-RUN = TILES // ROUNDS
-K_VECTOR = HEADS // 2
-JOBS_FIRST = 12
-EARLY_ROUNDS = 2
+VECTOR_HEADS = 3
+JOBS_FIRST = 13
 
 FLOPS = 2 * TOKENS * HID * 2 * F
 
@@ -190,67 +188,65 @@ def tile_rebasedlinearattention_pa_t_kernel(tc, hidden_states, Wq, Wk, gamma, be
             u[block, t] = u_pool.tile([P, F], F32, name="u")
             nc.gpsimd.tensor_add(out=by_head(u[block, t]), in0=by_head(scaled), in1=beta_all)
 
-        stats = {}
-        rstd = {}
-        shift = {}
-
-        def tiles_of(block, half):
-            return [(block, half), (block, 2 + half)]
-
-        def statistics(part):
-            stats[part] = small.tile([P, RUN * HEADS, 3], F32, name="stats")
-            for i, tile in enumerate(tiles_of(*part)):
+        def statistics(tiles, stats):
+            for i, tile in enumerate(tiles):
                 for h in range(0, HEADS, 2):
                     n = i * HEADS + h
                     nc.vector.bn_stats(
-                        out=stats[part][:, n : n + 2, :].rearrange("p n k -> p (n k)"),
+                        out=stats[:, n : n + 2, :].rearrange("p n k -> p (n k)"),
                         in_=u[tile][:, h * D : (h + 2) * D].rearrange("p (h d) -> p d h", h=2),
                     )
 
-        def inverse_deviation(part):
-            s = part[0] % 2
-            rstd[part] = small.tile([P, RUN * HEADS], F32, name="rstd")
-            nc.scalar.activation(
-                out=rstd[part][:],
-                in_=stats[part][:, :, 2],
-                func=ACT.Abs_reciprocal_sqrt,
-                scale=(1.0 if s == 0 else 1.0 / D),
-                bias=eps_col[:, s : s + 1],
-            )
-
-        def minus_mean_rstd(part):
-            shift[part] = small.tile([P, RUN * HEADS], F32, name="shift")
-            nc.vector.scalar_tensor_tensor(
-                out=shift[part][:], in0=stats[part][:, :, 1], scalar=-1.0, in1=rstd[part][:], op0=ALU.mult, op1=ALU.mult
-            )
-
-        def normalise_scalar(part, i, f, heads):
-            for h in heads:
-                n = i * HEADS + h
+        def inverse_deviation(tiles, stats, rstd):
+            for i, (block, t) in enumerate(tiles):
+                s = block % 2
+                rows = slice(i * HEADS, (i + 1) * HEADS)
                 nc.scalar.activation(
-                    out=f[:, h * D : (h + 1) * D],
-                    in_=u[tiles_of(*part)[i]][:, h * D : (h + 1) * D],
-                    func=ACT.Identity,
-                    scale=rstd[part][:, n : n + 1],
-                    bias=shift[part][:, n : n + 1],
+                    out=rstd[:, rows],
+                    in_=stats[:, rows, 2],
+                    func=ACT.Abs_reciprocal_sqrt,
+                    scale=(1.0 if s == 0 else 1.0 / D),
+                    bias=eps_col[:, s : s + 1],
                 )
 
-        def normalise_vector(part, i, f, heads):
-            for h in heads:
-                n = i * HEADS + h
-                nc.vector.tensor_scalar(
-                    out=f[:, h * D : (h + 1) * D],
-                    in0=u[tiles_of(*part)[i]][:, h * D : (h + 1) * D],
-                    scalar1=stats[part][:, n, 1:2],
-                    scalar2=rstd[part][:, n : n + 1],
-                    op0=ALU.subtract,
-                    op1=ALU.mult,
-                )
+        def minus_mean_rstd(tiles, stats, rstd):
+            shift = small.tile([P, 2 * HEADS], F32, name="shift")
+            rows = slice(0, len(tiles) * HEADS)
+            nc.vector.scalar_tensor_tensor(
+                out=shift[:, rows], in0=stats[:, rows, 1], scalar=-1.0, in1=rstd[:, rows], op0=ALU.mult, op1=ALU.mult
+            )
+            return shift
 
-        def store(part, i, f):
-            block, t = tiles_of(*part)[i]
-            g, s = divmod(block, 2)
-            nc.sync.dma_start(out=out_dram[s][g][:, t, :], in_=f[:])
+        def vector_heads(block, t):
+            if t < 2:
+                return HEADS if block == N_BLOCKS - 1 else 0
+            return VECTOR_HEADS
+
+        def normalise(tiles, stats, rstd, shift):
+            for i, (block, t) in enumerate(tiles):
+                g, s = divmod(block, 2)
+                f = f_pool.tile([P, F], F32, name="f")
+                for h in range(HEADS):
+                    n = i * HEADS + h
+                    cols = slice(h * D, (h + 1) * D)
+                    if h < vector_heads(block, t):
+                        nc.vector.tensor_scalar(
+                            out=f[:, cols],
+                            in0=u[block, t][:, cols],
+                            scalar1=stats[:, n, 1:2],
+                            scalar2=rstd[:, n : n + 1],
+                            op0=ALU.subtract,
+                            op1=ALU.mult,
+                        )
+                    else:
+                        nc.scalar.activation(
+                            out=f[:, cols],
+                            in_=u[block, t][:, cols],
+                            func=ACT.Identity,
+                            scale=rstd[:, n : n + 1],
+                            bias=shift[:, n : n + 1],
+                        )
+                nc.sync.dma_start(out=out_dram[s][g][:, t, :], in_=f[:])
 
         gb_all = const.tile([P, 2, D], F32)
         gb_col = const.tile([P, 2], F32)
@@ -276,37 +272,37 @@ def tile_rebasedlinearattention_pa_t_kernel(tc, hidden_states, Wq, Wk, gamma, be
 
         waiting = range(JOBS_FIRST, len(jobs))
         fresh = []
+        counted = None
+        inverted = None
         for r in range(N_ROUNDS + 5):
-            n_jobs = 2 if r < EARLY_ROUNDS else 1
-            transposed, waiting = waiting[:n_jobs], waiting[n_jobs:]
-            new, back, counted, inverted, last = (part_of_block(r - lag) for lag in (0, 2, 3, 4, 5))
+            transposed, waiting = waiting[:1], waiting[1:]
+            new, back = part_of_block(r), part_of_block(r - 2)
+            tiles = [(block, half) for block, half in part_of_block(r - 3)]
+            tiles += [(block, 2 + half) for block, half in part_of_block(r - 1)]
             for block, half in new:
                 project_tokens(block, 2 + half)
                 project_features(block, half)
             for block, half in back:
                 transpose_back(block, half)
-            for i, n in enumerate(transposed):
-                job_transpose(n, *job_pools[i])
-            for part in last:
-                minus_mean_rstd(part)
+            for n in transposed:
+                job_transpose(n, *job_pools[n % 2])
+            if inverted:
+                shift = minus_mean_rstd(*inverted)
             for block, half in new:
                 affine_tokens(block, 2 + half)
             for n in fresh:
                 job_quantise(n)
             fresh = transposed
-            for part in counted:
-                statistics(part)
-            for part in inverted:
-                inverse_deviation(part)
+            stats = small.tile([P, 2 * HEADS, 3], F32, name="stats")
+            statistics(tiles, stats)
+            if counted:
+                rstd = small.tile([P, 2 * HEADS], F32, name="rstd")
+                inverse_deviation(*counted, rstd)
             for part in new:
                 affine_features(*part)
-            f_of = [f_pool.tile([P, F], F32, name="f") for i in range(RUN * len(last))]
-            for part in last:
-                normalise_scalar(part, 0, f_of[0], range(HEADS))
-                store(part, 0, f_of[0])
+            if inverted:
+                normalise(*inverted, shift)
             for n in transposed:
                 job_group(n, nc.scalar.copy)
-            for part in last:
-                normalise_vector(part, 1, f_of[1], range(K_VECTOR))
-                normalise_scalar(part, 1, f_of[1], range(K_VECTOR, HEADS))
-                store(part, 1, f_of[1])
+            inverted = (*counted, rstd) if counted else None
+            counted = (tiles, stats) if tiles else None

@@ -29,7 +29,7 @@ ROUNDS = 2
 N_ROUNDS = ROUNDS * N_BLOCKS
 PAIR = HEADS // ROUNDS
 HALF = GROUP // 2
-VECTOR_HEADS = 3
+VECTOR_HEADS = {2: 2, 3: 3}
 JOBS_FIRST = 13
 
 FLOPS = 2 * TOKENS * HID * 2 * F
@@ -220,7 +220,7 @@ def tile_rebasedlinearattention_pa_t_kernel(tc, hidden_states, Wq, Wk, gamma, be
         def vector_heads(block, t):
             if t < 2:
                 return HEADS if block == N_BLOCKS - 1 else 0
-            return VECTOR_HEADS
+            return VECTOR_HEADS[t]
 
         def normalise(tiles, stats, rstd, shift):
             for i, (block, t) in enumerate(tiles):
@@ -286,10 +286,10 @@ def tile_rebasedlinearattention_pa_t_kernel(tc, hidden_states, Wq, Wk, gamma, be
                 transpose_back(block, half)
             for n in transposed:
                 job_transpose(n, *job_pools[n % 2])
-            if inverted:
-                shift = minus_mean_rstd(*inverted)
             for block, half in new:
                 affine_tokens(block, 2 + half)
+            if inverted:
+                shift = minus_mean_rstd(*inverted)
             for n in fresh:
                 job_quantise(n)
             fresh = transposed

@@ -29,7 +29,7 @@ ROUNDS = 2
 N_ROUNDS = ROUNDS * N_BLOCKS
 PAIR = HEADS // ROUNDS
 HALF = GROUP // 2
-VECTOR_HEADS = {2: 2, 3: 3}
+VECTOR_HEADS = 2
 JOBS_FIRST = 13
 
 FLOPS = 2 * TOKENS * HID * 2 * F
@@ -179,14 +179,11 @@ def tile_rebasedlinearattention_pa_t_kernel(tc, hidden_states, Wq, Wk, gamma, be
                     stop=(c == PASSES - 1),
                 )
 
-        def by_head(tile):
-            return tile[:].rearrange("p (h d) -> p h d", h=HEADS)
-
         def affine_tokens(block, t):
             scaled = scaled_pool.tile([P, F], F32, name="scaled")
-            nc.vector.tensor_mul(out=by_head(scaled), in0=by_head(acc_t[block, t]), in1=gamma_all)
+            nc.vector.tensor_mul(out=scaled[:], in0=acc_t[block, t][:], in1=gb_all[:, 0, :, :].rearrange("p h d -> p (h d)"))
             u[block, t] = u_pool.tile([P, F], F32, name="u")
-            nc.gpsimd.tensor_add(out=by_head(u[block, t]), in0=by_head(scaled), in1=beta_all)
+            nc.gpsimd.tensor_add(out=u[block, t][:], in0=scaled[:], in1=gb_all[:, 1, :, :].rearrange("p h d -> p (h d)"))
 
         def statistics(tiles, stats):
             for i, tile in enumerate(tiles):
@@ -220,7 +217,7 @@ def tile_rebasedlinearattention_pa_t_kernel(tc, hidden_states, Wq, Wk, gamma, be
         def vector_heads(block, t):
             if t < 2:
                 return HEADS if block == N_BLOCKS - 1 else 0
-            return VECTOR_HEADS[t]
+            return VECTOR_HEADS
 
         def normalise(tiles, stats, rstd, shift):
             for i, (block, t) in enumerate(tiles):
@@ -248,23 +245,27 @@ def tile_rebasedlinearattention_pa_t_kernel(tc, hidden_states, Wq, Wk, gamma, be
                         )
                 nc.sync.dma_start(out=out_dram[s][g][:, t, :], in_=f[:])
 
-        gb_all = const.tile([P, 2, D], F32)
+        gb_all = const.tile([P, 2, HEADS, D], F32)
         gb_col = const.tile([P, 2], F32)
-        gamma_all, beta_all = (gb_all[:, v, :].unsqueeze(1).to_broadcast([P, HEADS, D]) for v in range(2))
         for n in range(JOBS_FIRST):
             job_transpose(n, *job_pools[n % 3])
             job_group(n, nc.vector.tensor_copy if n % 2 == 0 else nc.scalar.copy)
             if n > 0:
                 job_quantise(n - 1)
             if n == 1:
-                gb_bank = mx_psum.tile([P, GROUP], F32, name="acc")
-                nc.tensor.matmul(out=gb_bank[:, 0 : 2 * D], lhsT=ones[:], rhs=gb_row[:], start=True, stop=True)
-                nc.scalar.copy(out=gb_all[:].rearrange("p v d -> p (v d)"), in_=gb_bank[:, 0 : 2 * D])
-            if n == 8:
-                col_bank = mx_psum.tile([P, GROUP], F32, name="acc")
+                gb_bank = mx_psum.tile([P, 2, D], F32, name="acc")
+                nc.tensor.matmul(
+                    out=gb_bank[:].rearrange("p v d -> p (v d)"), lhsT=ones[:], rhs=gb_row[:], start=True, stop=True
+                )
                 for v in range(2):
-                    nc.tensor.transpose(col_bank[:, v * P : (v + 1) * P], gb_all[:, v, :], ident[:])
-                    nc.scalar.copy(out=gb_col[:, v : v + 1], in_=col_bank[:, v * P : v * P + 1])
+                    nc.scalar.copy(
+                        out=gb_all[:, v, :, :], in_=gb_bank[:, v, :].unsqueeze(1).to_broadcast([P, HEADS, D])
+                    )
+            if n == 8:
+                col_bank = mx_psum.tile([P, 2, P], F32, name="acc")
+                for v in range(2):
+                    nc.tensor.transpose(col_bank[:, v, :], gb_all[:, v, 0, :], ident[:])
+                    nc.scalar.copy(out=gb_col[:, v : v + 1], in_=col_bank[:, v, 0:1])
         job_quantise(JOBS_FIRST - 1)
 
         def part_of_block(r):

from contextlib import ExitStack

import concourse.mybir as mybir
from concourse.masks import make_identity

F32 = mybir.dt.float32
BF16 = mybir.dt.bfloat16
U32 = mybir.dt.uint32
U8 = mybir.dt.uint8
FP8X4 = mybir.dt.float8_e4m3fn_x4
ALU = mybir.AluOpType
ACT = mybir.ActivationFunctionType

P = 128
TOKENS = 4 * 1024
HID = 1024
HEADS = 4
D = 128
F = HEADS * D
LN_EPS = 1e-5
K_PASS = 4 * P
PASSES = HID // K_PASS
WORDS = K_PASS // 2
GROUP = 512
N_GROUPS = TOKENS // GROUP
TILES = GROUP // P
N_BLOCKS = 2 * N_GROUPS
ROUNDS = 2
N_ROUNDS = ROUNDS * N_BLOCKS
PAIR = HEADS // ROUNDS
HALF = GROUP // 2
VECTOR_HEADS = 2
JOBS_FIRST = 13

FLOPS = 2 * TOKENS * HID * 2 * F


def tile_rebasedlinearattention_pa_t_kernel(tc, hidden_states, Wq, Wk, gamma, beta, out_0, out_1):
    nc = tc.nc
    x_dram = hidden_states.rearrange("b t k -> (b t) k").rearrange("(g p t) k -> g p t k", p=P, t=TILES)
    w_dram = [w.rearrange("(h p) k -> p h k", p=P) for w in (Wq, Wk)]
    out_dram = [
        o.rearrange("b t h d -> (b t) (h d)").rearrange("(g p t) f -> g p t f", p=P, t=TILES) for o in (out_0, out_1)
    ]

    with ExitStack() as stack:
        const = stack.enter_context(tc.tile_pool(name="const", bufs=1))
        raw_pool = stack.enter_context(tc.tile_pool(name="raw", bufs=16))
        grouped_pool = stack.enter_context(tc.tile_pool(name="grouped", bufs=6))
        ut_pool = stack.enter_context(tc.tile_pool(name="ut", bufs=3))
        scaled_pool = stack.enter_context(tc.tile_pool(name="scaled", bufs=3))
        u_pool = stack.enter_context(tc.tile_pool(name="u", bufs=8))
        f_pool = stack.enter_context(tc.tile_pool(name="f", bufs=8))
        small = stack.enter_context(tc.tile_pool(name="small", bufs=6))
        kt_psum = stack.enter_context(tc.psum_pool(name="kt", bufs=2))
        mx_psum = stack.enter_context(tc.psum_pool(name="mx", bufs=2))
        bt_psum = stack.enter_context(tc.psum_pool(name="bt", bufs=4))
        stack.enter_context(tc.manual_schedule())

        w_codes = const.tile([P, PASSES, 2 * F], U32, align_bytes=64)
        w_scales = const.tile([P, PASSES, 2 * F], U8, align_bytes=64)
        x_codes = const.tile([P, N_GROUPS, PASSES, GROUP], U32, align_bytes=64)
        x_scales = const.tile([P, N_GROUPS, PASSES, GROUP], U8, align_bytes=64)

        jobs = []

        def load_rows(rows_dram, codes, scales):
            raw = raw_pool.tile([P, 2, HID], BF16, name="raw")
            nc.sync.dma_start(out=raw[:], in_=rows_dram)
            for c in range(PASSES):
                jobs.append((raw[:].bitcast(F32), c, codes[:, c, :], scales[:, c, :]))

        def load_tokens(g, t):
            cols = slice(t * P, (t + 2) * P)
            load_rows(x_dram[g][:, t : t + 2, :], x_codes[:, g, :, cols], x_scales[:, g, :, cols])

        def load_weights(s):
            for h in range(0, HEADS, 2):
                cols = slice((s * HEADS + h) * D, (s * HEADS + h + 2) * D)
                load_rows(w_dram[s][:, h : h + 2, :], w_codes[:, :, cols], w_scales[:, :, cols])

        gb_row = const.tile([P, 2 * D], BF16)
        nc.vector.memset(gb_row[:], 0.0)
        load_tokens(0, 0)
        nc.sync.dma_start(out=gb_row[0:1, 0:D], in_=gamma.rearrange("(o d) -> o d", o=1))
        nc.sync.dma_start(out=gb_row[0:1, D : 2 * D], in_=beta.rearrange("(o d) -> o d", o=1))
        load_weights(0)
        load_tokens(0, 2)
        load_weights(1)
        for g in range(1, N_GROUPS):
            load_tokens(g, 0)
            load_tokens(g, 2)

        ident = const.tile([P, P], F32)
        make_identity(nc, ident[:])
        ones = const.tile([P, P], BF16)
        nc.vector.memset(ones[:], 1.0)
        eps_col = const.tile([P, 2], F32)
        nc.vector.memset(eps_col[:, 0:1], D * LN_EPS)
        nc.vector.memset(eps_col[:, 1:2], LN_EPS)
        warm = const.tile([P, 1], F32)
        nc.scalar.activation(out=warm[:], in_=eps_col[:, 0:1], func=ACT.Abs_reciprocal_sqrt)

        job_bank = {}
        job_grouped = {}
        job_pools = ((kt_psum, "kt"), (kt_psum, "kt"), (bt_psum, "bank"))

        def job_transpose(n, pool, name):
            words, c, codes, scales = jobs[n]
            job_bank[n] = pool.tile([P, 2, 2 * P], F32, name=name)
            for u in range(2):
                for r in range(2):
                    every_second = slice(c * WORDS + u, (c + 1) * WORDS, 2)
                    nc.tensor.transpose(job_bank[n][:, u, r * P : (r + 1) * P], words[:, r, every_second], ident[:])

        def job_group(n, engine_copy):
            job_grouped[n] = grouped_pool.tile([P, 2 * P, 4], BF16, align_bytes=64, name="grouped")
            engine_copy(out=job_grouped[n][:].bitcast(F32), in_=job_bank[n][:].rearrange("p u r -> p r u"))

        def job_quantise(n):
            words, c, codes, scales = jobs[n]
            nc.vector.quantize_mx(
                out=codes.bitcast(FP8X4), scales=scales, in_=job_grouped[n][:].rearrange("p r t -> p (r t)")
            )

        u = {}

        u_t = {}
        acc_f = {}

        def project_features(block, half):
            g, s = divmod(block, 2)
            acc_f[block, half] = mx_psum.tile([P, PAIR, HALF], F32, name="acc")
            for i in range(PAIR):
                head = s * HEADS + PAIR * half + i
                cols = slice(head * D, (head + 1) * D)
                for c in range(PASSES):
                    nc.tensor.matmul_mx(
                        out=acc_f[block, half][:, i, :],
                        lhsT=w_codes[:, c, cols].bitcast(FP8X4),
                        lhsT_scale=w_scales[:, c, cols],
                        rhs=x_codes[:, g, c, 0:HALF].bitcast(FP8X4),
                        rhs_scale=x_scales[:, g, c, 0:HALF],
                        start=(c == 0),
                        stop=(c == PASSES - 1),
                    )

        def affine_features(block, half):
            if half == 0:
                u_t[block] = ut_pool.tile([P, HEADS, HALF], F32, name="u_t")
            nc.scalar.activation(
                out=u_t[block][:, PAIR * half : PAIR * (half + 1), :],
                in_=acc_f[block, half][:],
                func=ACT.Identity,
                scale=gb_col[:, 0:1],
                bias=gb_col[:, 1:2],
            )

        def transpose_back(block, t):
            u[block, t] = bt_psum.tile([P, F], F32, name="bank")
            for h in range(HEADS):
                nc.tensor.transpose(u[block, t][:, h * D : (h + 1) * D], u_t[block][:, h, t * P : (t + 1) * P], ident[:])

        acc_t = {}

        def project_tokens(block, t):
            g, s = divmod(block, 2)
            rows = slice(t * P, (t + 1) * P)
            cols = slice(s * F, (s + 1) * F)
            acc_t[block, t] = mx_psum.tile([P, F], F32, name="acc")
            for c in range(PASSES):
                nc.tensor.matmul_mx(
                    out=acc_t[block, t][:],
                    lhsT=x_codes[:, g, c, rows].bitcast(FP8X4),
                    lhsT_scale=x_scales[:, g, c, rows],
                    rhs=w_codes[:, c, cols].bitcast(FP8X4),
                    rhs_scale=w_scales[:, c, cols],
                    start=(c == 0),
                    stop=(c == PASSES - 1),
                )

        def affine_tokens(block, t):
            scaled = scaled_pool.tile([P, F], F32, name="scaled")
            nc.vector.tensor_mul(out=scaled[:], in0=acc_t[block, t][:], in1=gb_all[:, 0, :, :].rearrange("p h d -> p (h d)"))
            u[block, t] = u_pool.tile([P, F], F32, name="u")
            nc.gpsimd.tensor_add(out=u[block, t][:], in0=scaled[:], in1=gb_all[:, 1, :, :].rearrange("p h d -> p (h d)"))

        def statistics(tiles, stats):
            for i, tile in enumerate(tiles):
                for h in range(0, HEADS, 2):
                    n = i * HEADS + h
                    nc.vector.bn_stats(
                        out=stats[:, n : n + 2, :].rearrange("p n k -> p (n k)"),
                        in_=u[tile][:, h * D : (h + 2) * D].rearrange("p (h d) -> p d h", h=2),
                    )

        def inverse_deviation(tiles, stats, rstd):
            for i, (block, t) in enumerate(tiles):
                s = block % 2
                rows = slice(i * HEADS, (i + 1) * HEADS)
                nc.scalar.activation(
                    out=rstd[:, rows],
                    in_=stats[:, rows, 2],
                    func=ACT.Abs_reciprocal_sqrt,
                    scale=(1.0 if s == 0 else 1.0 / D),
                    bias=eps_col[:, s : s + 1],
                )

        def minus_mean_rstd(tiles, stats, rstd):
            shift = small.tile([P, 2 * HEADS], F32, name="shift")
            rows = slice(0, len(tiles) * HEADS)
            nc.vector.scalar_tensor_tensor(
                out=shift[:, rows], in0=stats[:, rows, 1], scalar=-1.0, in1=rstd[:, rows], op0=ALU.mult, op1=ALU.mult
            )
            return shift

        def vector_heads(block, t):
            if t < 2:
                return HEADS if block == N_BLOCKS - 1 else 0
            return VECTOR_HEADS

        def normalise(tiles, stats, rstd, shift):
            for i, (block, t) in enumerate(tiles):
                g, s = divmod(block, 2)
                f = f_pool.tile([P, F], F32, name="f")
                for h in range(HEADS):
                    n = i * HEADS + h
                    cols = slice(h * D, (h + 1) * D)
                    if h < vector_heads(block, t):
                        nc.vector.tensor_scalar(
                            out=f[:, cols],
                            in0=u[block, t][:, cols],
                            scalar1=stats[:, n, 1:2],
                            scalar2=rstd[:, n : n + 1],
                            op0=ALU.subtract,
                            op1=ALU.mult,
                        )
                    else:
                        nc.scalar.activation(
                            out=f[:, cols],
                            in_=u[block, t][:, cols],
                            func=ACT.Identity,
                            scale=rstd[:, n : n + 1],
                            bias=shift[:, n : n + 1],
                        )
                nc.sync.dma_start(out=out_dram[s][g][:, t, :], in_=f[:])

        gb_all = const.tile([P, 2, HEADS, D], F32)
        gb_col = const.tile([P, 2], F32)
        for n in range(JOBS_FIRST):
            job_transpose(n, *job_pools[n % 3])
            job_group(n, nc.vector.tensor_copy if n % 2 == 0 else nc.scalar.copy)
            if n > 0:
                job_quantise(n - 1)
            if n == 1:
                gb_bank = mx_psum.tile([P, 2, D], F32, name="acc")
                nc.tensor.matmul(
                    out=gb_bank[:].rearrange("p v d -> p (v d)"), lhsT=ones[:], rhs=gb_row[:], start=True, stop=True
                )
                for v in range(2):
                    nc.scalar.copy(
                        out=gb_all[:, v, :, :], in_=gb_bank[:, v, :].unsqueeze(1).to_broadcast([P, HEADS, D])
                    )
            if n == 8:
                col_bank = mx_psum.tile([P, 2, P], F32, name="acc")
                for v in range(2):
                    nc.tensor.transpose(col_bank[:, v, :], gb_all[:, v, 0, :], ident[:])
                    nc.scalar.copy(out=gb_col[:, v : v + 1], in_=col_bank[:, v, 0:1])
        job_quantise(JOBS_FIRST - 1)

        def part_of_block(r):
            return [divmod(r, ROUNDS)] if 0 <= r < N_ROUNDS else []

        waiting = range(JOBS_FIRST, len(jobs))
        fresh = []
        counted = None
        inverted = None
        for r in range(N_ROUNDS + 5):
            transposed, waiting = waiting[:1], waiting[1:]
            new, back = part_of_block(r), part_of_block(r - 2)
            tiles = [(block, half) for block, half in part_of_block(r - 3)]
            tiles += [(block, 2 + half) for block, half in part_of_block(r - 1)]
            for block, half in new:
                project_tokens(block, 2 + half)
                project_features(block, half)
            for block, half in back:
                transpose_back(block, half)
            for n in transposed:
                job_transpose(n, *job_pools[n % 2])
            for block, half in new:
                affine_tokens(block, 2 + half)
            if inverted:
                shift = minus_mean_rstd(*inverted)
            for n in fresh:
                job_quantise(n)
            fresh = transposed
            stats = small.tile([P, 2 * HEADS, 3], F32, name="stats")
            statistics(tiles, stats)
            if counted:
                rstd = small.tile([P, 2 * HEADS], F32, name="rstd")
                inverse_deviation(*counted, rstd)
            for part in new:
                affine_features(*part)
            if inverted:
                normalise(*inverted, shift)
            for n in transposed:
                job_group(n, nc.scalar.copy)
            inverted = (*counted, rstd) if counted else None
            counted = (tiles, stats) if tiles else None
